import numpy as np
import ml_dtypes


def mxq(x, axis, fmt="e4m3"):
    dtype, down = {"e4m3": (ml_dtypes.float8_e4m3fn, 7), "e5m2": (ml_dtypes.float8_e5m2, 14)}[fmt]
    v = np.moveaxis(np.asarray(x, np.float32).astype(ml_dtypes.bfloat16).astype(np.float64), axis, -1)
    blocks = v.reshape(v.shape[:-1] + (-1, 32))
    amax = np.abs(blocks).max(-1, keepdims=True)
    byte = np.maximum(np.where(amax > 0, np.frexp(amax)[1] - 1 + 127, 0) - down, 1)
    scale = np.exp2(byte - 127.0)
    codes = (blocks / scale).astype(np.float32).astype(dtype).astype(np.float64)
    return np.moveaxis((codes * scale).reshape(v.shape), -1, axis)


WIDE = False


def mx_kscale(k):
    if not WIDE:
        return np.ones(k)
    levels = np.array([10, -10, 5, -5, 0])
    if k % 512:
        return np.exp2(np.random.permutation(np.resize(levels, k // 32))).repeat(32)
    a = np.empty((k // 512, 16))
    for p in range(k // 512):
        a[p, :8] = np.random.permutation(np.resize(levels, 8))
        for g in range(8):
            far = levels[np.abs(levels - a[p, g]) >= 10]
            a[p, g + 8] = far[np.random.randint(len(far))]
    return np.exp2(a.ravel()).repeat(32)


BF16 = ml_dtypes.bfloat16


def bf(x):
    return np.asarray(x, np.float32).astype(BF16)


def f64(x):
    return np.asarray(x).astype(np.float64)


E2M1 = np.array([0.0, 0.5, 1.0, 1.5, 2.0, 3.0, 4.0, 6.0, -0.0, -0.5, -1.0, -1.5, -2.0, -3.0, -4.0, -6.0])


def pack_weight(w, fmt):
    k, n = w.shape
    w = f64(bf(w)).reshape(k // 32, 32, n)
    amax = np.abs(w).max(1)
    if fmt == "e4m3":
        byte = np.frexp(amax)[1] - 1 + 127 - 7
    else:
        mant, ex = np.frexp(amax / 6.0)
        byte = np.where(mant > 0.5, ex, ex - 1) + 127
    byte = np.clip(np.where(amax > 0, byte, 1), 1, 254)
    scaled = (w * np.exp2(127.0 - byte)[:, None, :]).reshape(k, n).astype(np.float32)
    by_word = np.ascontiguousarray(scaled.reshape(k // 512, 128, 4, n).transpose(0, 1, 3, 2))
    if fmt == "e4m3":
        words = by_word.astype(ml_dtypes.float8_e4m3fn).view(np.uint8)
    else:
        c = by_word.astype(ml_dtypes.float4_e2m1fn).view(np.uint8) & 0xF
        words = c[..., 0::2] | (c[..., 1::2] << 4)
    return np.ascontiguousarray(words), np.ascontiguousarray(byte.astype(np.uint8).reshape(k // 512, 16, n))


def unpack_weight(words, scales, fmt):
    g, p, n, _ = words.shape
    if fmt == "e4m3":
        vals = np.ascontiguousarray(words).view(ml_dtypes.float8_e4m3fn).astype(np.float64)
    else:
        nib = np.empty((g, p, n, 4), np.uint8)
        nib[..., 0::2] = words & 0xF
        nib[..., 1::2] = words >> 4
        vals = E2M1[nib]
    vals = vals * np.repeat(np.exp2(scales.astype(np.float64) - 127.0), 8, axis=1)[..., None]
    return vals.transpose(0, 1, 3, 2).reshape(g * 512, n)


B, S, HID, NH, HD, RD, KVC, QC = 2, 256, 2048, 16, 128, 64, 512, 1536


def heads(t, d):
    return t.reshape(B, S, NH, d).transpose(0, 2, 1, 3)


def rope(t):
    R = t.shape[-1]
    inv_freq = 1.0 / (10000.0 ** (np.arange(0, R, 2) / R))
    ang = np.arange(t.shape[-2])[:, None] * inv_freq[None, :]
    cos, sin = np.cos(ang), np.sin(ang)
    t1, t2 = t[..., : R // 2], t[..., R // 2:]
    return np.concatenate([t1 * cos - t2 * sin, t2 * cos + t1 * sin], axis=-1)


def draw0():
    s, t = mx_kscale(HID), mx_kscale(QC)
    x = bf(np.random.standard_normal((B, S, HID)) * s)
    W_qd_words, W_qd_scales = pack_weight(np.random.standard_normal((HID, QC)) / np.sqrt(HID) / s[:, None] * t, "e4m3")
    b_qd = bf(np.random.standard_normal(QC) * 0.3 * t)
    W_qu_words, W_qu_scales = pack_weight(np.random.standard_normal((QC, NH * HD)) / np.sqrt(QC) / t[:, None], "e4m3")
    b_qu = bf(np.random.standard_normal(NH * HD) * 0.3)
    W_qr_words, W_qr_scales = pack_weight(np.random.standard_normal((QC, NH * RD)) / np.sqrt(QC) / t[:, None], "e4m3")
    b_qr = bf(np.random.standard_normal(NH * RD) * 0.3)
    return {"x": x,
            "W_qd_words": W_qd_words,
            "W_qd_scales": W_qd_scales,
            "b_qd": b_qd,
            "W_qu_words": W_qu_words,
            "W_qu_scales": W_qu_scales,
            "b_qu": b_qu,
            "W_qr_words": W_qr_words,
            "W_qr_scales": W_qr_scales,
            "b_qr": b_qr}


def core(x, W_qd_words, W_qd_scales, b_qd, W_qu_words, W_qu_scales, b_qu, W_qr_words, W_qr_scales, b_qr):
    q_c = (mxq(f64(x), 2, "e4m3") @ unpack_weight(W_qd_words, W_qd_scales, "e4m3")) + f64(b_qd)
    cq = mxq(q_c, 2, "e4m3")
    queries_c = heads((cq @ unpack_weight(W_qu_words, W_qu_scales, "e4m3")) + f64(b_qu), HD)
    queries_r = rope(heads((cq @ unpack_weight(W_qr_words, W_qr_scales, "e4m3")) + f64(b_qr), RD))
    return np.concatenate([queries_c, queries_r], axis=-1)


def e4m3fn_bytes(y):
    return np.clip(np.asarray(y, np.float64), -448.0, 448.0).astype(np.float32).astype(ml_dtypes.float8_e4m3fn).view(np.uint8)


def e4m3fn_values(b):
    return np.asarray(b, np.uint8).view(ml_dtypes.float8_e4m3fn).astype(np.float64)


def setup_inputs():
    d = draw0()
    x0 = np.asarray(d['x']).astype(np.float64)
    s = (np.max(np.abs(x0), axis=(0, 1), keepdims=True) / 448.0).astype(np.float32)
    out = {}
    for k, v in d.items():
        if k == 'x':
            out['x_bytes'] = e4m3fn_bytes(x0 / s.astype(np.float64))
            out['x_scale'] = s
        else:
            out[k] = v
    return out


def reference(x_bytes, x_scale, W_qd_words, W_qd_scales, b_qd, W_qu_words, W_qu_scales, b_qu, W_qr_words, W_qr_scales, b_qr):
    return core(e4m3fn_values(x_bytes) * x_scale.astype(np.float64), W_qd_words, W_qd_scales, b_qd, W_qu_words, W_qu_scales, b_qu, W_qr_words, W_qr_scales, b_qr)

@@ -1,0 +1,425 @@
+import math
+from contextlib import ExitStack
+
+import concourse.mybir as mybir
+from concourse.masks import make_identity
+
+F32 = mybir.dt.float32
+BF16 = mybir.dt.bfloat16
+I32 = mybir.dt.int32
+U32 = mybir.dt.uint32
+U8 = mybir.dt.uint8
+FP8 = mybir.dt.float8_e4m3fn
+FP8X4 = mybir.dt.float8_e4m3fn_x4
+ADD = mybir.AluOpType.add
+SUB = mybir.AluOpType.subtract
+MULT = mybir.AluOpType.mult
+SIN = mybir.ActivationFunctionType.Sin
+COPY = mybir.ActivationFunctionType.Copy
+
+P = 128
+B, S, HID, NH, HD, RD, QC = 2, 256, 2048, 16, 128, 64, 1536
+NT = S // P
+GX = HID // 512
+GC = QC // 512
+HALF = RD // 2
+
+FLOPS = 2 * B * S * (HID * QC + QC * NH * (HD + RD))
+
+
+def tile_multiheadlatentattention_pb_w8_kernel(
+    tc, x_bytes, x_scale, W_qd_words, W_qd_scales, b_qd, W_qu_words, W_qu_scales, b_qu,
+    W_qr_words, W_qr_scales, b_qr, out,
+):
+    nc = tc.nc
+    with ExitStack() as ctx:
+        keep = ctx.enter_context(tc.tile_pool(name="keep", bufs=1))
+        stage = ctx.enter_context(tc.tile_pool(name="stage", bufs=2))
+        accp = ctx.enter_context(tc.psum_pool(name="accp", bufs=1))
+        turnp = ctx.enter_context(tc.psum_pool(name="turnp", bufs=2))
+        ctx.enter_context(tc.manual_schedule())
+
+        pos = keep.tile([P, NT], F32, name="pos")
+        nc.gpsimd.iota(pos[:], pattern=[[1, NT]], base=0, channel_multiplier=NT,
+                       allow_small_or_imprecise_dtypes=True)
+        warm = keep.tile([P, 1], F32, name="warm")
+        nc.scalar.activation(warm[:], pos[:, 0:1], SIN, scale=0.0)
+        ident = keep.tile([P, P], F32, name="ident")
+        make_identity(nc, ident[:])
+
+        qd_planes = keep.tile([P, QC], U8, name="qd_planes", align_bytes=64)
+        qu_planes = keep.tile([P, NH * HD], U8, name="qu_planes", align_bytes=64)
+        qr_planes = keep.tile([P, NH * RD], U8, name="qr_planes", align_bytes=64)
+        sc_rows = keep.tile([P, 512], F32, name="sc_rows")
+        nc.vector.memset(sc_rows[:], 0.0)
+        nc.vector.memset(qd_planes[:].bitcast(I32), 0)
+        nc.vector.memset(qr_planes[:].bitcast(I32), 0)
+        nc.vector.memset(qu_planes[:].bitcast(I32), 0)
+
+        sc = keep.tile([P, GX, 4], F32, name="sc")
+
+        x8 = [[keep.tile([P, NT, 1024], U8, name="x8_%d%d" % (b, h)) for h in range(2)] for b in range(B)]
+
+        def load_x(b, h):
+            nc.sync.dma_start(
+                out=x8[b][h][:],
+                in_=x_bytes[b].rearrange("(p i) k -> p i k", i=NT)[:, :, 1024 * h : 1024 * (h + 1)],
+            )
+
+        def load_planes(planes, scales, groups):
+            for q in range(4):
+                nc.sync.dma_start(
+                    out=planes[32 * q : 32 * q + 4 * groups, :].bitcast(I32),
+                    in_=scales[:, 4 * q : 4 * q + 4, :].bitcast(I32),
+                )
+
+        def load_words(words, g, width, name):
+            w = keep.tile([P, width], U32, name=name, align_bytes=64)
+            nc.sync.dma_start(out=w[:].bitcast(I32), in_=words[g].rearrange("p n t -> p (n t)").bitcast(I32))
+            return w
+
+        def load_bias(bias, width, name):
+            t = keep.tile([P, width], BF16, name=name)
+            nc.sync.dma_start(out=t[:], in_=bias.partition_broadcast(P))
+            return t
+
+        load_x(0, 0)
+        nc.sync.dma_start(out=sc_rows[0:GX, :], in_=x_scale.rearrange("a o (g k) -> (a o g) k", g=GX))
+        load_planes(qd_planes, W_qd_scales, GX)
+        w_qd = [load_words(W_qd_words, 0, QC, "w_qd0")]
+        load_x(0, 1)
+        w_qd.append(load_words(W_qd_words, 1, QC, "w_qd1"))
+        load_x(1, 0)
+        w_qd.append(load_words(W_qd_words, 2, QC, "w_qd2"))
+        load_x(1, 1)
+        w_qd.append(load_words(W_qd_words, 3, QC, "w_qd3"))
+        bd = load_bias(b_qd, QC, "bd")
+        load_planes(qr_planes, W_qr_scales, GC)
+        load_planes(qu_planes, W_qu_scales, GC)
+        br = load_bias(b_qr, NH * RD, "br")
+        w_qr = [load_words(W_qr_words, g, NH * RD, "w_qr%d" % g) for g in range(GC)]
+        bu = load_bias(b_qu, NH * HD, "bu")
+        w_qu = [load_words(W_qu_words, g, NH * HD, "w_qu%d" % g) for g in range(GC)]
+
+        turns = keep.tile([P, NT, HALF], F32, name="turns")
+        nc.gpsimd.tensor_scalar(turns[:, :, 0:1], pos[:].unsqueeze(2), 1.0 / (2.0 * math.pi), None, MULT)
+        width = 1
+        while width < HALF:
+            nc.gpsimd.tensor_scalar(turns[:, :, width : 2 * width], turns[:, :, 0:width],
+                                    10000.0 ** (-width / HALF), None, MULT)
+            width *= 2
+        phase = keep.tile([P, 2, NT, HALF], F32, name="phase")
+        nc.gpsimd.tensor_scalar(phase[:, 0], turns[:], 0.25, None, ADD)
+        nc.gpsimd.tensor_scalar(phase[:, 1], turns[:], 0.0, None, ADD)
+        whole_i = keep.tile([P, 2, NT, HALF], I32, name="whole_i")
+        whole = keep.tile([P, 2, NT, HALF], F32, name="whole")
+        frac = keep.tile([P, 2, NT, HALF], F32, name="frac")
+        cos_t = keep.tile([P, NT, 2, HALF], F32, name="cos_t")
+        sin_t = keep.tile([P, NT, 2, HALF], F32, name="sin_t")
+
+        xb = [[keep.tile([P, NT, 1024], BF16, name="xb_%d%d" % (b, h), align_bytes=64) for h in range(2)] for b in range(B)]
+
+        def cast(engine, b, g):
+            h, cols = g // 2, slice(512 * (g % 2), 512 * (g % 2) + 512)
+            for i in range(NT):
+                src, dst = x8[b][h][:, i, cols].bitcast(FP8), xb[b][h][:, i, cols]
+                if engine == "v":
+                    nc.vector.tensor_copy(out=dst, in_=src)
+                else:
+                    nc.scalar.copy(out=dst, in_=src)
+
+        def turn_x(b, g):
+            turned = turnp.tile([P, 2, NT * P], F32, name="turned")
+            for i in range(NT):
+                words = xb[b][g // 2][:, i, :].bitcast(F32)
+                for u in range(2):
+                    lo = 256 * (g % 2)
+                    nc.tensor.transpose(turned[:, u, i * P : (i + 1) * P], words[:, lo + u : lo + 256 : 2], ident[:])
+            return turned
+
+        def scale_x(b, g, turned):
+            xg = stage.tile([P, NT * P, 4], BF16, name="xg", bufs=3, align_bytes=64)
+            nc.vector.tensor_tensor(
+                xg[:].rearrange("p r (u e) -> p r u e", u=2),
+                turned[:].rearrange("p u r -> p (u r)").bitcast(BF16).rearrange("p (u r e) -> p r u e", u=2, e=2),
+                sc[:, g, :].rearrange("p (u e) -> p u e", u=2).unsqueeze(1).to_broadcast([P, NT * P, 2, 2]),
+                MULT,
+            )
+            return xg
+
+        def scale_x_gpsimd(b, g, turned):
+            xw = stage.tile([P, NT * P, 4], BF16, name="xw", align_bytes=64)
+            nc.scalar.copy(out=xw[:].rearrange("p r k -> p (r k)").bitcast(F32).rearrange("p (r u) -> p r u", u=2),
+                           in_=turned[:].rearrange("p u r -> p r u"))
+            xg = stage.tile([P, NT * P, 4], BF16, name="xg", bufs=3, align_bytes=64)
+            nc.gpsimd.tensor_tensor(xg[:], xw[:], sc[:, g, :].unsqueeze(1).to_broadcast([P, NT * P, 4]), MULT)
+            return xg
+
+        def quantize(grouped, name):
+            codes = keep.tile([P, NT * P], U32, name="q" + name, align_bytes=64)
+            plane = keep.tile([P, NT * P], U8, name="s" + name, align_bytes=64)
+            nc.vector.quantize_mx(out=codes[:].bitcast(FP8X4), scales=plane[:],
+                                  in_=grouped[:].rearrange("p r k -> p (r k)"))
+            return codes, plane
+
+        def mx(acc, codes, plane, i, words, planes, g, cols, start, stop):
+            rows = slice(i * P, (i + 1) * P)
+            nc.tensor.matmul_mx(out=acc[:], lhsT=codes[:, rows].bitcast(FP8X4), lhsT_scale=plane[:, rows],
+                                rhs=words[:, cols].bitcast(FP8X4), rhs_scale=planes[4 * g :, cols],
+                                start=start, stop=stop)
+
+        def new_acc(slot):
+            acc = accp.tile([P, 512], F32, name="acc%d" % slot)
+            return acc
+
+        def mm_x(b, g, tiles=(0, 1)):
+            for i in tiles:
+                for n in range(GC):
+                    if g == 0:
+                        accs[i, n] = new_acc(i * GC + n)
+                    codes, plane = xq[b, g]
+                    mx(accs[i, n], codes, plane, i, w_qd[g], qd_planes, g, slice(512 * n, 512 * n + 512), g == 0, g == GX - 1)
+
+        def c_exit(b, i, n, by_vector):
+            if (b, n) not in c_bf:
+                c_bf[b, n] = keep.tile([P, NT, 512], BF16, name="c%d%d" % (b, n), align_bytes=64)
+            dst = c_bf[b, n][:, i, :].rearrange("p (u k e) -> p u k e", u=2, e=2)
+            bias = bd[:, 512 * n : 512 * n + 512].rearrange("p (k u e) -> p u k e", u=2, e=2)
+            src = accs[i, n]
+            if by_vector:
+                nc.vector.tensor_tensor(dst, src[:].rearrange("p (k u e) -> p u k e", u=2, e=2), bias, ADD)
+            else:
+                raw = stage.tile([P, 512], F32, name="c_raw", bufs=3)
+                nc.scalar.copy(out=raw[:], in_=src[:])
+                nc.gpsimd.tensor_tensor(dst, raw[:].rearrange("p (k u e) -> p u k e", u=2, e=2), bias, ADD)
+
+        def turn_c(b, n):
+            turned = turnp.tile([P, 2, NT * P], F32, name="turned")
+            for i in range(NT):
+                for u in range(2):
+                    nc.tensor.transpose(turned[:, u, i * P : (i + 1) * P],
+                                        c_bf[b, n][:, i, 256 * u : 256 * u + 256].bitcast(F32), ident[:])
+            cg = stage.tile([P, NT * P, 4], BF16, name="cg", bufs=3, align_bytes=64)
+            nc.scalar.copy(out=cg[:].rearrange("p r k -> p (r k)").bitcast(F32).rearrange("p (r u) -> p r u", u=2),
+                           in_=turned[:].rearrange("p u r -> p r u"))
+            return cg
+
+        results = {}
+
+        def group2(b, i, kind, n, slot):
+            acc = new_acc(slot) if slot < 6 else turnp.tile([P, 512], F32, name="turned")
+            words, planes = (w_qr, qr_planes) if kind == "r" else (w_qu, qu_planes)
+            for g in range(GC):
+                codes, plane = cq[b, g]
+                mx(acc, codes, plane, i, words[g], planes, g, slice(512 * n, 512 * n + 512), g == 0, g == GC - 1)
+            return acc
+
+        def exit_u(b, i, n, acc):
+            nc.vector.tensor_tensor(results[b][:, 4 * n : 4 * n + 4, i, 0:HD], acc[:].rearrange("p (h d) -> p h d", d=HD),
+                                    bu[:, 512 * n : 512 * n + 512].rearrange("p (h d) -> p h d", d=HD), ADD)
+
+        q, ca, sa = {}, {}, {}
+        slots = [0]
+
+        def group_r(b, i, n, slot):
+            acc = group2(b, i, "r", n, slot)
+            if n == 0:
+                q[b, i] = stage.tile([P, NH, 2, HALF], F32, name="q_rot")
+            nc.vector.tensor_tensor(q[b, i][:, 8 * n : 8 * n + 8].rearrange("p h a j -> p (h a j)"), acc[:],
+                                    br[:, 512 * n : 512 * n + 512], ADD)
+
+        def products_scalar(b, i, lo, hi):
+            if lo == 0:
+                ca[b, i] = stage.tile([P, HALF, NH, 2], F32, name="ca")
+                sa[b, i] = stage.tile([P, HALF, NH, 2], F32, name="sa")
+            for j in range(lo, hi):
+                for dst, table in ((ca, cos_t), (sa, sin_t)):
+                    nc.scalar.activation(dst[b, i][:, j], q[b, i][:, :, :, j], COPY, scale=table[:, i, 1, j : j + 1])
+
+        def sums_scalar(b, i, eng):
+            for a, op in ((0, SUB), (1, ADD)):
+                eng.tensor_tensor(results[b][:, :, i, HD + HALF * a : HD + HALF * (a + 1)],
+                                  ca[b, i][:, :, :, a].rearrange("p j h -> p h j"),
+                                  sa[b, i][:, :, :, 1 - a].rearrange("p j h -> p h j"), op)
+
+        def products_gpsimd(b, i, n, eng):
+            if n == 0:
+                ca[b, i] = stage.tile([P, NH, 2, HALF], F32, name="ca")
+                sa[b, i] = stage.tile([P, NH, 2, HALF], F32, name="sa")
+            hs = slice(8 * n, 8 * n + 8)
+            eng.tensor_tensor(ca[b, i][:, hs].rearrange("p h a j -> p h (a j)"), q[b, i][:, hs].rearrange("p h a j -> p h (a j)"),
+                              cos_t[:, i].rearrange("p a j -> p (a j)").unsqueeze(1).to_broadcast([P, 8, RD]), MULT)
+            for a in range(2):
+                eng.tensor_tensor(sa[b, i][:, hs, a, :], q[b, i][:, hs, 1 - a, :],
+                                  sin_t[:, i, a, :].unsqueeze(1).to_broadcast([P, 8, HALF]), MULT)
+
+        def sums_gpsimd(b, i, n, eng):
+            hs = slice(8 * n, 8 * n + 8)
+            eng.tensor_tensor(results[b][:, hs, i, HD:], ca[b, i][:, hs].rearrange("p h a j -> p h (a j)"),
+                              sa[b, i][:, hs].rearrange("p h a j -> p h (a j)"), ADD)
+
+        def store(b, h0, h1):
+            nc.sync.dma_start(out=out[b, h0:h1].rearrange("h (p i) d -> p h (i d)", i=NT),
+                              in_=results[b][:, h0:h1].rearrange("p h i d -> p h (i d)"))
+
+        accs, xq, c_bf, cq, xt, xg = {}, {}, {}, {}, {}, {}
+
+        def T(b, g):
+            xt[b, g] = turn_x(b, g)
+
+        def E(b, g):
+            xg[b, g] = scale_x(b, g, xt[b, g])
+
+        def EG(b, g):
+            xg[b, g] = scale_x_gpsimd(b, g, xt[b, g])
+
+        def Q(b, g):
+            xq[b, g] = quantize(xg[b, g], "x%d%d" % (b, g))
+
+        cg = {}
+
+        def TC(b, n):
+            cg[b, n] = turn_c(b, n)
+
+        def QCn(b, n):
+            cq[b, n] = quantize(cg[b, n], "c%d%d" % (b, n))
+
+        def CX(b, i, n, how):
+            c_exit(b, i, n, how == "v")
+
+        def U(b, n):
+            for i in range(NT):
+                acc = group2(b, i, "u", n, SLOTS[slots[0] % 6])
+                slots[0] += 1
+                exit_u(b, i, n, acc)
+
+        def tables():
+            nc.scalar.activation(cos_t[:], frac[:, 0].unsqueeze(2).to_broadcast([P, NT, 2, HALF]), SIN, scale=2.0 * math.pi)
+            nc.scalar.activation(sin_t[:, :, 0], frac[:, 1], SIN, scale=-2.0 * math.pi)
+            nc.scalar.activation(sin_t[:, :, 1], frac[:, 1], SIN, scale=2.0 * math.pi)
+
+        def SCALES():
+            turned = turnp.tile([P, 4, P], F32, name="turned")
+            for t in range(4):
+                nc.tensor.transpose(turned[:, t, :], sc_rows[:, t::4], ident[:])
+            nc.vector.tensor_copy(out=sc[:], in_=turned[:, :, 0:GX].rearrange("p t g -> p g t"))
+
+        def PS(b, i, lo, hi):
+            products_scalar(b, i, lo, hi)
+
+        def PG(b, i, n):
+            products_gpsimd(b, i, n, nc.gpsimd)
+
+        results[0] = keep.tile([P, NH, NT, HD + RD], F32, name="res0")
+        results[1] = keep.tile([P, NH, NT, HD + RD], F32, name="res1")
+        SLOTS = [0, 3, 1, 4, 2, 5]
+        V, G = nc.vector, nc.gpsimd
+
+        SCALES()
+        cast("v",0,0)
+        cast("s",0,1)
+        T(0,0)
+        E(0,0)
+        T(0,1)
+        Q(0,0)
+        E(0,1)
+        cast("s",0,3)
+        cast("v",0,2)
+        mm_x(0,0)
+        Q(0,1)
+        T(0,2)
+        T(0,3)
+        E(0,2)
+        cast("s",1,0)
+        mm_x(0,1)
+        EG(0,3)
+        Q(0,2)
+        cast("s",1,1)
+        T(1,0)
+        T(1,1)
+        cast("s",1,2)
+        mm_x(0,2)
+        E(1,0)
+        Q(0,3)
+        cast("s",1,3)
+        E(1,1)
+        Q(1,0)
+        Q(1,1)
+        V.tensor_copy(out=whole_i[:], in_=phase[:])
+        V.tensor_copy(out=whole[:], in_=whole_i[:])
+        V.tensor_tensor(frac[:], phase[:], whole[:], SUB)
+        mm_x(0,3)
+        T(1,2)
+        T(1,3)
+        CX(0,0,0,"v")
+        CX(0,0,1,"s")
+        CX(0,0,2,"v")
+        CX(0,1,0,"s")
+        CX(0,1,1,"v")
+        CX(0,1,2,"v")
+        E(1,2)
+        EG(1,3)
+        tables()
+        mm_x(1,0)
+        Q(1,2)
+        TC(0,0)
+        TC(0,1)
+        QCn(0,0)
+        mm_x(1,1,(0,))
+        QCn(0,1)
+        TC(0,2)
+        QCn(0,2)
+        mm_x(1,1,(1,))
+        Q(1,3)
+        group_r(0,0,0,6)
+        group_r(0,0,1,6)
+        PS(0,0,0,16)
+        group_r(0,1,0,6)
+        group_r(0,1,1,6)
+        mm_x(1,2)
+        PG(0,1,0)
+        mm_x(1,3)
+        CX(1,0,0,"v")
+        CX(1,1,0,"s")
+        CX(1,0,1,"v")
+        CX(1,1,1,"v")
+        U(0,0)
+        CX(1,0,2,"s")
+        CX(1,1,2,"v")
+        TC(1,0)
+        PS(0,0,16,24)
+        TC(1,1)
+        PG(0,1,1)
+        QCn(1,0)
+        QCn(1,1)
+        U(0,1)
+        TC(1,2)
+        QCn(1,2)
+        PS(0,0,24,32)
+        sums_scalar(0,0,G)
+        sums_gpsimd(0,1,0,V)
+        store(0,0,4)
+        sums_gpsimd(0,1,1,V)
+        store(0,4,8)
+        group_r(1,0,0,6)
+        group_r(1,0,1,6)
+        PS(1,0,0,32)
+        group_r(1,1,0,6)
+        PG(1,1,0)
+        group_r(1,1,1,6)
+        PG(1,1,1)
+        U(0,2)
+        store(0,8,12)
+        U(0,3)
+        store(0,12,16)
+        U(1,0)
+        sums_scalar(1,0,G)
+        sums_gpsimd(1,1,0,V)
+        store(1,0,4)
+        U(1,1)
+        sums_gpsimd(1,1,1,V)
+        store(1,4,8)
+        U(1,2)
+        store(1,8,12)
+        U(1,3)
+        store(1,12,16)

@@ -35,7 +35,7 @@ def tile_multiheadlatentattention_pb_w8_kernel(
     with ExitStack() as ctx:
         keep = ctx.enter_context(tc.tile_pool(name="keep", bufs=1))
         stage = ctx.enter_context(tc.tile_pool(name="stage", bufs=2))
-        accp = ctx.enter_context(tc.psum_pool(name="accp", bufs=1))
+        accp = ctx.enter_context(tc.psum_pool(name="accp", bufs=6))
         turnp = ctx.enter_context(tc.psum_pool(name="turnp", bufs=2))
         ctx.enter_context(tc.manual_schedule())
 
@@ -48,13 +48,17 @@ def tile_multiheadlatentattention_pb_w8_kernel(
         make_identity(nc, ident[:])
 
         qd_planes = keep.tile([P, QC], U8, name="qd_planes", align_bytes=64)
-        qu_planes = keep.tile([P, NH * HD], U8, name="qu_planes", align_bytes=64)
-        qr_planes = keep.tile([P, NH * RD], U8, name="qr_planes", align_bytes=64)
+        qu_planes = keep.tile([P, GC, NH * HD], U8, name="qu_planes", align_bytes=64)
+        qr_planes = keep.tile([P, GC, NH * RD], U8, name="qr_planes", align_bytes=64)
+        bias_rows = keep.tile([P, 512], BF16, name="bias_rows")
+        ident_b = keep.tile([P, P], BF16, name="ident_b")
         sc_rows = keep.tile([P, 512], F32, name="sc_rows")
         nc.vector.memset(sc_rows[:], 0.0)
         nc.vector.memset(qd_planes[:].bitcast(I32), 0)
-        nc.vector.memset(qr_planes[:].bitcast(I32), 0)
-        nc.vector.memset(qu_planes[:].bitcast(I32), 0)
+        nc.vector.memset(bias_rows[:], 0.0)
+        nc.vector.tensor_copy(out=ident_b[:], in_=ident[:])
+        nc.vector.memset(qr_planes[:].rearrange("p g n -> p (g n)").bitcast(I32), 0)
+        nc.vector.memset(qu_planes[:].rearrange("p g n -> p (g n)").bitcast(I32), 0)
 
         sc = keep.tile([P, GX, 4], F32, name="sc")
 
@@ -78,28 +82,39 @@ def tile_multiheadlatentattention_pb_w8_kernel(
             nc.sync.dma_start(out=w[:].bitcast(I32), in_=words[g].rearrange("p n t -> p (n t)").bitcast(I32))
             return w
 
-        def load_bias(bias, width, name):
-            t = keep.tile([P, width], BF16, name=name)
-            nc.sync.dma_start(out=t[:], in_=bias.partition_broadcast(P))
-            return t
+        def load_block_planes(planes, scales):
+            for q in range(4):
+                nc.sync.dma_start(out=planes[32 * q : 32 * q + 4].bitcast(I32),
+                                  in_=scales[:, 4 * q : 4 * q + 4, :].rearrange("g q n -> q g n").bitcast(I32))
+
+        def load_bias(bias, row, rows):
+            nc.sync.dma_start(out=bias_rows[row : row + rows, 0 : bias.shape[0] // rows], in_=bias.rearrange("(r c) -> r c", r=rows))
 
         load_x(0, 0)
         nc.sync.dma_start(out=sc_rows[0:GX, :], in_=x_scale.rearrange("a o (g k) -> (a o g) k", g=GX))
         load_planes(qd_planes, W_qd_scales, GX)
         w_qd = [load_words(W_qd_words, 0, QC, "w_qd0")]
         load_x(0, 1)
+        load_bias(b_qd, 0, 4)
         w_qd.append(load_words(W_qd_words, 1, QC, "w_qd1"))
         load_x(1, 0)
         w_qd.append(load_words(W_qd_words, 2, QC, "w_qd2"))
         load_x(1, 1)
         w_qd.append(load_words(W_qd_words, 3, QC, "w_qd3"))
-        bd = load_bias(b_qd, QC, "bd")
-        load_planes(qr_planes, W_qr_scales, GC)
-        load_planes(qu_planes, W_qu_scales, GC)
-        br = load_bias(b_qr, NH * RD, "br")
+        load_bias(b_qu, 4, 4)
+        load_bias(b_qr, 8, 2)
+        load_block_planes(qr_planes, W_qr_scales)
         w_qr = [load_words(W_qr_words, g, NH * RD, "w_qr%d" % g) for g in range(GC)]
-        bu = load_bias(b_qu, NH * HD, "bu")
-        w_qu = [load_words(W_qu_words, g, NH * HD, "w_qu%d" % g) for g in range(GC)]
+        load_block_planes(qu_planes, W_qu_scales)
+        w_qu = []
+        for h in range(2):
+            w = keep.tile([P, GC, 1024], U32, name="w_qu%d" % h, align_bytes=64)
+            nc.sync.dma_start(out=w[:].bitcast(I32),
+                              in_=W_qu_words[:, :, 1024 * h : 1024 * (h + 1), :].rearrange("g p n t -> p g (n t)").bitcast(I32))
+            w_qu.append(w)
+        bd = keep.tile([P, QC], BF16, name="bd")
+        bu = keep.tile([P, NH * HD], BF16, name="bu")
+        br = keep.tile([P, NH * RD], BF16, name="br")
 
         turns = keep.tile([P, NT, HALF], F32, name="turns")
         nc.gpsimd.tensor_scalar(turns[:, :, 0:1], pos[:].unsqueeze(2), 1.0 / (2.0 * math.pi), None, MULT)
@@ -118,8 +133,38 @@ def tile_multiheadlatentattention_pb_w8_kernel(
         sin_t = keep.tile([P, NT, 2, HALF], F32, name="sin_t")
 
         xb = [[keep.tile([P, NT, 1024], BF16, name="xb_%d%d" % (b, h), align_bytes=64) for h in range(2)] for b in range(B)]
+        turned, lifted, grouped, xq, cq, accs, c_raw, c_bf = {}, {}, {}, {}, {}, {}, {}, {}
+        q, ca, sa = {}, {}, {}
+        results = [keep.tile([P, NH, NT, HD + RD], F32, name="res%d" % b) for b in range(B)]
+        V, G, S_ = nc.vector, nc.gpsimd, nc.scalar
 
-        def cast(engine, b, g):
+        def new_turned():
+            bank = turnp.tile([P, 512], F32, name="bank")
+            return bank
+
+        def new_acc():
+            acc = accp.tile([P, 512], F32, name="acc")
+            return acc
+
+        def scales_turn():
+            turned["s"] = new_turned()
+            for t in range(4):
+                nc.tensor.transpose(turned["s"][:, P * t : P * t + P], sc_rows[:, t::4], ident[:])
+
+        def scales_copy():
+            nc.vector.tensor_copy(out=sc[:], in_=turned["s"][:].rearrange("p (t g) -> p g t", t=4)[:, 0:GX, :])
+
+        def spread(row):
+            turned["b", row] = new_turned()
+            cols = 384 if row < 4 else 512
+            nc.tensor.matmul(turned["b", row][:, 0:cols], lhsT=ident_b[:, row : row + 1].to_broadcast([P, P]),
+                             rhs=bias_rows[:, 0:cols], start=True, stop=True)
+
+        def spread_copy(row):
+            tile, first, cols = (bd, 0, 384) if row < 4 else (bu, 4, 512) if row < 8 else (br, 8, 512)
+            nc.scalar.copy(out=tile[:, (row - first) * cols : (row - first + 1) * cols], in_=turned["b", row][:, 0:cols])
+
+        def cast(b, g, engine):
             h, cols = g // 2, slice(512 * (g % 2), 512 * (g % 2) + 512)
             for i in range(NT):
                 src, dst = x8[b][h][:, i, cols].bitcast(FP8), xb[b][h][:, i, cols]
@@ -128,122 +173,136 @@ def tile_multiheadlatentattention_pb_w8_kernel(
                 else:
                     nc.scalar.copy(out=dst, in_=src)
 
-        def turn_x(b, g):
-            turned = turnp.tile([P, 2, NT * P], F32, name="turned")
+        def x_turn(b, g):
+            turned[b, g] = new_turned()
+            lo = 256 * (g % 2)
             for i in range(NT):
                 words = xb[b][g // 2][:, i, :].bitcast(F32)
                 for u in range(2):
-                    lo = 256 * (g % 2)
-                    nc.tensor.transpose(turned[:, u, i * P : (i + 1) * P], words[:, lo + u : lo + 256 : 2], ident[:])
-            return turned
+                    nc.tensor.transpose(turned[b, g][:, 256 * u + P * i : 256 * u + P * i + P], words[:, lo + u : lo + 256 : 2], ident[:])
 
-        def scale_x(b, g, turned):
-            xg = stage.tile([P, NT * P, 4], BF16, name="xg", bufs=3, align_bytes=64)
+        def x_scale_v(b, g):
+            grouped[b, g] = stage.tile([P, NT * P, 4], BF16, name="xg", bufs=3, align_bytes=64)
             nc.vector.tensor_tensor(
-                xg[:].rearrange("p r (u e) -> p r u e", u=2),
-                turned[:].rearrange("p u r -> p (u r)").bitcast(BF16).rearrange("p (u r e) -> p r u e", u=2, e=2),
+                grouped[b, g][:].rearrange("p r (u e) -> p r u e", u=2),
+                turned[b, g][:].bitcast(BF16).rearrange("p (u r e) -> p r u e", u=2, e=2),
                 sc[:, g, :].rearrange("p (u e) -> p u e", u=2).unsqueeze(1).to_broadcast([P, NT * P, 2, 2]),
                 MULT,
             )
-            return xg
 
-        def scale_x_gpsimd(b, g, turned):
-            xw = stage.tile([P, NT * P, 4], BF16, name="xw", align_bytes=64)
-            nc.scalar.copy(out=xw[:].rearrange("p r k -> p (r k)").bitcast(F32).rearrange("p (r u) -> p r u", u=2),
-                           in_=turned[:].rearrange("p u r -> p r u"))
-            xg = stage.tile([P, NT * P, 4], BF16, name="xg", bufs=3, align_bytes=64)
-            nc.gpsimd.tensor_tensor(xg[:], xw[:], sc[:, g, :].unsqueeze(1).to_broadcast([P, NT * P, 4]), MULT)
-            return xg
+        def words_out(dst, bank):
+            nc.scalar.copy(out=dst[:].rearrange("p r k -> p (r k)").bitcast(F32).rearrange("p (r u) -> p r u", u=2),
+                           in_=bank[:].rearrange("p (u r) -> p r u", u=2))
 
-        def quantize(grouped, name):
+        def x_lift(b, g):
+            lifted[b, g] = stage.tile([P, NT * P, 4], BF16, name="xw", align_bytes=64)
+            words_out(lifted[b, g], turned[b, g])
+
+        def x_scale_g(b, g):
+            grouped[b, g] = stage.tile([P, NT * P, 4], BF16, name="xg", bufs=3, align_bytes=64)
+            nc.gpsimd.tensor_tensor(grouped[b, g][:], lifted[b, g][:], sc[:, g, :].unsqueeze(1).to_broadcast([P, NT * P, 4]), MULT)
+
+        def quantize(tile, name):
             codes = keep.tile([P, NT * P], U32, name="q" + name, align_bytes=64)
             plane = keep.tile([P, NT * P], U8, name="s" + name, align_bytes=64)
-            nc.vector.quantize_mx(out=codes[:].bitcast(FP8X4), scales=plane[:],
-                                  in_=grouped[:].rearrange("p r k -> p (r k)"))
+            nc.vector.quantize_mx(out=codes[:].bitcast(FP8X4), scales=plane[:], in_=tile[:].rearrange("p r k -> p (r k)"))
             return codes, plane
 
-        def mx(acc, codes, plane, i, words, planes, g, cols, start, stop):
+        def x_quant(b, g):
+            xq[b, g] = quantize(grouped[b, g], "x%d%d" % (b, g))
+
+        def mx(acc, operand, i, words, word_plane, start, stop):
+            codes, plane = operand
             rows = slice(i * P, (i + 1) * P)
             nc.tensor.matmul_mx(out=acc[:], lhsT=codes[:, rows].bitcast(FP8X4), lhsT_scale=plane[:, rows],
-                                rhs=words[:, cols].bitcast(FP8X4), rhs_scale=planes[4 * g :, cols],
-                                start=start, stop=stop)
+                                rhs=words.bitcast(FP8X4), rhs_scale=word_plane, start=start, stop=stop)
 
-        def new_acc(slot):
-            acc = accp.tile([P, 512], F32, name="acc%d" % slot)
-            return acc
+        def x_mm(b, g, i):
+            for n in range(GC):
+                if (b, i, n) not in accs:
+                    accs[b, i, n] = new_acc()
+                cols = slice(512 * n, 512 * n + 512)
+                mx(accs[b, i, n], xq[b, g], i, w_qd[g][:, cols], qd_planes[4 * g :, cols], g == 0, g == GX - 1)
 
-        def mm_x(b, g, tiles=(0, 1)):
-            for i in tiles:
-                for n in range(GC):
-                    if g == 0:
-                        accs[i, n] = new_acc(i * GC + n)
-                    codes, plane = xq[b, g]
-                    mx(accs[i, n], codes, plane, i, w_qd[g], qd_planes, g, slice(512 * n, 512 * n + 512), g == 0, g == GX - 1)
-
-        def c_exit(b, i, n, by_vector):
+        def c_views(b, i, n):
             if (b, n) not in c_bf:
                 c_bf[b, n] = keep.tile([P, NT, 512], BF16, name="c%d%d" % (b, n), align_bytes=64)
-            dst = c_bf[b, n][:, i, :].rearrange("p (u k e) -> p u k e", u=2, e=2)
-            bias = bd[:, 512 * n : 512 * n + 512].rearrange("p (k u e) -> p u k e", u=2, e=2)
-            src = accs[i, n]
-            if by_vector:
-                nc.vector.tensor_tensor(dst, src[:].rearrange("p (k u e) -> p u k e", u=2, e=2), bias, ADD)
-            else:
-                raw = stage.tile([P, 512], F32, name="c_raw", bufs=3)
-                nc.scalar.copy(out=raw[:], in_=src[:])
-                nc.gpsimd.tensor_tensor(dst, raw[:].rearrange("p (k u e) -> p u k e", u=2, e=2), bias, ADD)
+            return (c_bf[b, n][:, i, :].rearrange("p (u k e) -> p u k e", u=2, e=2),
+                    bd[:, 512 * n : 512 * n + 512].rearrange("p (k u e) -> p u k e", u=2, e=2))
 
-        def turn_c(b, n):
-            turned = turnp.tile([P, 2, NT * P], F32, name="turned")
-            for i in range(NT):
+        def c_add_v(b, i, n):
+            dst, bias = c_views(b, i, n)
+            nc.vector.tensor_tensor(dst, accs[b, i, n][:].rearrange("p (k u e) -> p u k e", u=2, e=2), bias, ADD)
+
+        def c_lift(b, i, n):
+            c_raw[b, i, n] = stage.tile([P, 512], F32, name="c_raw", bufs=3)
+            nc.scalar.copy(out=c_raw[b, i, n][:], in_=accs[b, i, n][:])
+
+        def c_add_g(b, i, n):
+            dst, bias = c_views(b, i, n)
+            nc.gpsimd.tensor_tensor(dst, c_raw[b, i, n][:].rearrange("p (k u e) -> p u k e", u=2, e=2), bias, ADD)
+
+        def c_turn(b, k):
+            turned["c", b, k] = new_turned()
+            for s, (i, n) in enumerate(GROUPS[b][k]):
                 for u in range(2):
-                    nc.tensor.transpose(turned[:, u, i * P : (i + 1) * P],
+                    nc.tensor.transpose(turned["c", b, k][:, 256 * s + P * u : 256 * s + P * u + P],
                                         c_bf[b, n][:, i, 256 * u : 256 * u + 256].bitcast(F32), ident[:])
-            cg = stage.tile([P, NT * P, 4], BF16, name="cg", bufs=3, align_bytes=64)
-            nc.scalar.copy(out=cg[:].rearrange("p r k -> p (r k)").bitcast(F32).rearrange("p (r u) -> p r u", u=2),
-                           in_=turned[:].rearrange("p u r -> p r u"))
-            return cg
 
-        results = {}
+        def c_copy(b, k):
+            count = len(GROUPS[b][k])
+            grouped["c", b, k] = stage.tile([P, count * P, 4], BF16, name="cg%d" % count, bufs=3, align_bytes=64)
+            nc.scalar.copy(
+                out=grouped["c", b, k][:].rearrange("p r k -> p (r k)").bitcast(F32).rearrange("p (c r u) -> p c r u", c=count, u=2),
+                in_=turned["c", b, k][:, 0 : 256 * count].rearrange("p (c u r) -> p c r u", c=count, u=2))
 
-        def group2(b, i, kind, n, slot):
-            acc = new_acc(slot) if slot < 6 else turnp.tile([P, 512], F32, name="turned")
-            words, planes = (w_qr, qr_planes) if kind == "r" else (w_qu, qu_planes)
+        def c_quant(b, k):
+            count = len(GROUPS[b][k])
+            codes = keep.tile([P, count * P], U32, name="qc%d%d" % (b, k), align_bytes=64)
+            plane = keep.tile([P, count * P], U8, name="sc%d%d" % (b, k), align_bytes=64)
+            nc.vector.quantize_mx(out=codes[:].bitcast(FP8X4), scales=plane[:], in_=grouped["c", b, k][:].rearrange("p r k -> p (r k)"))
+            for s, (i, n) in enumerate(GROUPS[b][k]):
+                cq[b, i, n] = (codes, plane), s
+
+        def u_mm(b, n, i):
+            accs["u", b, n, i] = new_acc()
+            cols, half = slice(512 * n, 512 * n + 512), slice(512 * (n % 2), 512 * (n % 2) + 512)
             for g in range(GC):
-                codes, plane = cq[b, g]
-                mx(acc, codes, plane, i, words[g], planes, g, slice(512 * n, 512 * n + 512), g == 0, g == GC - 1)
-            return acc
+                operand, s = cq[b, i, g]
+                mx(accs["u", b, n, i], operand, s, w_qu[n // 2][:, g, half], qu_planes[:, g, cols], g == 0, g == GC - 1)
 
-        def exit_u(b, i, n, acc):
-            nc.vector.tensor_tensor(results[b][:, 4 * n : 4 * n + 4, i, 0:HD], acc[:].rearrange("p (h d) -> p h d", d=HD),
+        def u_add(b, n, i):
+            nc.vector.tensor_tensor(results[b][:, 4 * n : 4 * n + 4, i, 0:HD], accs["u", b, n, i][:].rearrange("p (h d) -> p h d", d=HD),
                                     bu[:, 512 * n : 512 * n + 512].rearrange("p (h d) -> p h d", d=HD), ADD)
 
-        q, ca, sa = {}, {}, {}
-        slots = [0]
+        def r_mm(b, n, i):
+            accs["r", b, n, i] = new_turned()
+            cols = slice(512 * n, 512 * n + 512)
+            for g in range(GC):
+                operand, s = cq[b, i, g]
+                mx(accs["r", b, n, i], operand, s, w_qr[g][:, cols], qr_planes[:, g, cols], g == 0, g == GC - 1)
 
-        def group_r(b, i, n, slot):
-            acc = group2(b, i, "r", n, slot)
-            if n == 0:
+        def r_add(b, n, i):
+            if (b, i) not in q:
                 q[b, i] = stage.tile([P, NH, 2, HALF], F32, name="q_rot")
-            nc.vector.tensor_tensor(q[b, i][:, 8 * n : 8 * n + 8].rearrange("p h a j -> p (h a j)"), acc[:],
+            nc.vector.tensor_tensor(q[b, i][:, 8 * n : 8 * n + 8].rearrange("p h a j -> p (h a j)"), accs["r", b, n, i][:],
                                     br[:, 512 * n : 512 * n + 512], ADD)
 
-        def products_scalar(b, i, lo, hi):
-            if lo == 0:
+        def prod_s(b, i, lo, hi):
+            if (b, i) not in ca:
                 ca[b, i] = stage.tile([P, HALF, NH, 2], F32, name="ca")
                 sa[b, i] = stage.tile([P, HALF, NH, 2], F32, name="sa")
             for j in range(lo, hi):
                 for dst, table in ((ca, cos_t), (sa, sin_t)):
                     nc.scalar.activation(dst[b, i][:, j], q[b, i][:, :, :, j], COPY, scale=table[:, i, 1, j : j + 1])
 
-        def sums_scalar(b, i, eng):
-            for a, op in ((0, SUB), (1, ADD)):
-                eng.tensor_tensor(results[b][:, :, i, HD + HALF * a : HD + HALF * (a + 1)],
-                                  ca[b, i][:, :, :, a].rearrange("p j h -> p h j"),
-                                  sa[b, i][:, :, :, 1 - a].rearrange("p j h -> p h j"), op)
+        def sum_s(b, i, a, eng):
+            eng.tensor_tensor(results[b][:, :, i, HD + HALF * a : HD + HALF * (a + 1)],
+                              ca[b, i][:, :, :, a].rearrange("p j h -> p h j"),
+                              sa[b, i][:, :, :, 1 - a].rearrange("p j h -> p h j"), ADD if a else SUB)
 
-        def products_gpsimd(b, i, n, eng):
-            if n == 0:
+        def prod_g(b, i, n, eng):
+            if (b, i) not in ca:
                 ca[b, i] = stage.tile([P, NH, 2, HALF], F32, name="ca")
                 sa[b, i] = stage.tile([P, NH, 2, HALF], F32, name="sa")
             hs = slice(8 * n, 8 * n + 8)
@@ -253,173 +312,232 @@ def tile_multiheadlatentattention_pb_w8_kernel(
                 eng.tensor_tensor(sa[b, i][:, hs, a, :], q[b, i][:, hs, 1 - a, :],
                                   sin_t[:, i, a, :].unsqueeze(1).to_broadcast([P, 8, HALF]), MULT)
 
-        def sums_gpsimd(b, i, n, eng):
+        def sum_g(b, i, n, eng):
             hs = slice(8 * n, 8 * n + 8)
             eng.tensor_tensor(results[b][:, hs, i, HD:], ca[b, i][:, hs].rearrange("p h a j -> p h (a j)"),
                               sa[b, i][:, hs].rearrange("p h a j -> p h (a j)"), ADD)
 
-        def store(b, h0, h1):
-            nc.sync.dma_start(out=out[b, h0:h1].rearrange("h (p i) d -> p h (i d)", i=NT),
-                              in_=results[b][:, h0:h1].rearrange("p h i d -> p h (i d)"))
-
-        accs, xq, c_bf, cq, xt, xg = {}, {}, {}, {}, {}, {}
-
-        def T(b, g):
-            xt[b, g] = turn_x(b, g)
-
-        def E(b, g):
-            xg[b, g] = scale_x(b, g, xt[b, g])
-
-        def EG(b, g):
-            xg[b, g] = scale_x_gpsimd(b, g, xt[b, g])
-
-        def Q(b, g):
-            xq[b, g] = quantize(xg[b, g], "x%d%d" % (b, g))
-
-        cg = {}
-
-        def TC(b, n):
-            cg[b, n] = turn_c(b, n)
-
-        def QCn(b, n):
-            cq[b, n] = quantize(cg[b, n], "c%d%d" % (b, n))
-
-        def CX(b, i, n, how):
-            c_exit(b, i, n, how == "v")
-
-        def U(b, n):
-            for i in range(NT):
-                acc = group2(b, i, "u", n, SLOTS[slots[0] % 6])
-                slots[0] += 1
-                exit_u(b, i, n, acc)
+        def angles(k):
+            if k == 0:
+                nc.vector.tensor_copy(out=whole_i[:], in_=phase[:])
+            elif k == 1:
+                nc.vector.tensor_copy(out=whole[:], in_=whole_i[:])
+            else:
+                nc.vector.tensor_tensor(frac[:], phase[:], whole[:], SUB)
 
         def tables():
             nc.scalar.activation(cos_t[:], frac[:, 0].unsqueeze(2).to_broadcast([P, NT, 2, HALF]), SIN, scale=2.0 * math.pi)
             nc.scalar.activation(sin_t[:, :, 0], frac[:, 1], SIN, scale=-2.0 * math.pi)
             nc.scalar.activation(sin_t[:, :, 1], frac[:, 1], SIN, scale=2.0 * math.pi)
 
-        def SCALES():
-            turned = turnp.tile([P, 4, P], F32, name="turned")
-            for t in range(4):
-                nc.tensor.transpose(turned[:, t, :], sc_rows[:, t::4], ident[:])
-            nc.vector.tensor_copy(out=sc[:], in_=turned[:, :, 0:GX].rearrange("p t g -> p g t"))
+        def store(b, i, h0, h1):
+            nc.sync.dma_start(out=out[b, h0:h1].rearrange("h (p i) d -> p i h d", i=NT)[:, i], in_=results[b][:, h0:h1, i, :])
 
-        def PS(b, i, lo, hi):
-            products_scalar(b, i, lo, hi)
+        GROUPS = [[[(0, 0), (1, 0)], [(0, 1), (1, 1)], [(0, 2), (1, 2)]],
+                  [[(0, 0), (0, 1)], [(0, 2)], [(1, 0), (1, 1)], [(1, 2)]]]
 
-        def PG(b, i, n):
-            products_gpsimd(b, i, n, nc.gpsimd)
-
-        results[0] = keep.tile([P, NH, NT, HD + RD], F32, name="res0")
-        results[1] = keep.tile([P, NH, NT, HD + RD], F32, name="res1")
-        SLOTS = [0, 3, 1, 4, 2, 5]
-        V, G = nc.vector, nc.gpsimd
-
-        SCALES()
-        cast("v",0,0)
-        cast("s",0,1)
-        T(0,0)
-        E(0,0)
-        T(0,1)
-        Q(0,0)
-        E(0,1)
-        cast("s",0,3)
-        cast("v",0,2)
-        mm_x(0,0)
-        Q(0,1)
-        T(0,2)
-        T(0,3)
-        E(0,2)
-        cast("s",1,0)
-        mm_x(0,1)
-        EG(0,3)
-        Q(0,2)
-        cast("s",1,1)
-        T(1,0)
-        T(1,1)
-        cast("s",1,2)
-        mm_x(0,2)
-        E(1,0)
-        Q(0,3)
-        cast("s",1,3)
-        E(1,1)
-        Q(1,0)
-        Q(1,1)
-        V.tensor_copy(out=whole_i[:], in_=phase[:])
-        V.tensor_copy(out=whole[:], in_=whole_i[:])
-        V.tensor_tensor(frac[:], phase[:], whole[:], SUB)
-        mm_x(0,3)
-        T(1,2)
-        T(1,3)
-        CX(0,0,0,"v")
-        CX(0,0,1,"s")
-        CX(0,0,2,"v")
-        CX(0,1,0,"s")
-        CX(0,1,1,"v")
-        CX(0,1,2,"v")
-        E(1,2)
-        EG(1,3)
+        cast(0,1,"s")
+        scales_turn()
+        cast(0,0,"v")
+        cast(0,3,"s")
+        x_turn(0,0)
+        scales_copy()
+        x_scale_v(0,0)
+        x_turn(0,1)
+        angles(0)
+        x_quant(0,0)
+        cast(0,2,"v")
+        x_mm(0,0,0)
+        x_mm(0,0,1)
+        x_turn(0,3)
+        x_lift(0,3)
+        x_scale_v(0,1)
+        cast(1,1,"s")
+        x_quant(0,1)
+        x_turn(0,2)
+        cast(1,0,"s")
+        x_mm(0,1,0)
+        x_mm(0,1,1)
+        x_turn(1,1)
+        x_scale_v(0,2)
+        x_quant(0,2)
+        x_turn(1,0)
+        cast(1,3,"s")
+        x_mm(0,2,0)
+        x_mm(0,2,1)
+        x_scale_v(1,1)
+        cast(1,2,"s")
+        x_scale_g(0,3)
+        x_scale_v(1,0)
+        x_quant(0,3)
+        spread(1)
+        spread(0)
+        x_quant(1,1)
+        spread_copy(1)
+        x_mm(0,3,0)
+        spread(2)
+        spread_copy(0)
+        c_add_v(0,0,0)
+        c_lift(0,0,1)
+        spread(3)
+        spread_copy(3)
+        spread_copy(2)
+        x_mm(0,3,1)
+        x_quant(1,0)
+        x_turn(1,3)
+        x_lift(1,3)
+        x_turn(1,2)
+        c_add_v(0,1,2)
+        c_add_v(0,0,2)
+        c_turn(0,2)
+        c_lift(0,1,0)
+        x_scale_v(1,2)
+        c_add_g(0,1,0)
+        x_mm(1,0,0)
+        spread(7)
+        c_add_g(0,0,1)
+        c_copy(0,2)
+        spread_copy(7)
+        angles(1)
+        spread(5)
+        x_mm(1,1,0)
+        spread_copy(5)
+        spread(9)
+        x_scale_g(1,3)
+        spread(4)
+        c_add_v(0,1,1)
+        x_mm(1,0,1)
+        spread_copy(9)
+        spread_copy(4)
+        x_quant(1,2)
+        angles(2)
+        c_turn(0,1)
+        c_copy(0,1)
+        c_turn(0,0)
+        c_quant(0,2)
+        c_quant(0,1)
+        x_mm(1,2,0)
+        x_quant(1,3)
+        c_copy(0,0)
+        spread(6)
+        c_quant(0,0)
+        spread(8)
+        x_mm(1,3,0)
+        spread_copy(6)
+        r_mm(0,1,0)
         tables()
-        mm_x(1,0)
-        Q(1,2)
-        TC(0,0)
-        TC(0,1)
-        QCn(0,0)
-        mm_x(1,1,(0,))
-        QCn(0,1)
-        TC(0,2)
-        QCn(0,2)
-        mm_x(1,1,(1,))
-        Q(1,3)
-        group_r(0,0,0,6)
-        group_r(0,0,1,6)
-        PS(0,0,0,16)
-        group_r(0,1,0,6)
-        group_r(0,1,1,6)
-        mm_x(1,2)
-        PG(0,1,0)
-        mm_x(1,3)
-        CX(1,0,0,"v")
-        CX(1,1,0,"s")
-        CX(1,0,1,"v")
-        CX(1,1,1,"v")
-        U(0,0)
-        CX(1,0,2,"s")
-        CX(1,1,2,"v")
-        TC(1,0)
-        PS(0,0,16,24)
-        TC(1,1)
-        PG(0,1,1)
-        QCn(1,0)
-        QCn(1,1)
-        U(0,1)
-        TC(1,2)
-        QCn(1,2)
-        PS(0,0,24,32)
-        sums_scalar(0,0,G)
-        sums_gpsimd(0,1,0,V)
-        store(0,0,4)
-        sums_gpsimd(0,1,1,V)
-        store(0,4,8)
-        group_r(1,0,0,6)
-        group_r(1,0,1,6)
-        PS(1,0,0,32)
-        group_r(1,1,0,6)
-        PG(1,1,0)
-        group_r(1,1,1,6)
-        PG(1,1,1)
-        U(0,2)
-        store(0,8,12)
-        U(0,3)
-        store(0,12,16)
-        U(1,0)
-        sums_scalar(1,0,G)
-        sums_gpsimd(1,1,0,V)
-        store(1,0,4)
-        U(1,1)
-        sums_gpsimd(1,1,1,V)
-        store(1,4,8)
-        U(1,2)
-        store(1,8,12)
-        U(1,3)
-        store(1,12,16)
+        c_add_v(1,0,2)
+        spread_copy(8)
+        r_mm(0,0,0)
+        c_lift(1,0,1)
+        r_add(0,1,0)
+        r_add(0,0,0)
+        prod_s(0,0,16,20)
+        c_add_v(1,0,0)
+        r_mm(0,1,1)
+        prod_s(0,0,20,24)
+        r_mm(0,0,1)
+        x_mm(1,1,1)
+        x_mm(1,2,1)
+        r_add(0,1,1)
+        x_mm(1,3,1)
+        prod_s(0,0,8,12)
+        r_add(0,0,1)
+        u_mm(0,3,1)
+        c_add_v(1,1,2)
+        prod_s(0,0,28,32)
+        u_mm(0,2,1)
+        prod_s(0,0,4,8)
+        c_add_g(1,0,1)
+        c_lift(1,1,1)
+        prod_s(0,0,12,16)
+        c_turn(1,1)
+        prod_g(0,1,1,G)
+        sum_g(0,1,1,V)
+        u_add(0,3,1)
+        c_turn(1,0)
+        u_mm(0,1,1)
+        prod_g(0,1,0,G)
+        prod_s(0,0,0,4)
+        c_add_v(1,1,0)
+        u_mm(0,1,0)
+        c_copy(1,1)
+        u_mm(0,3,0)
+        c_add_g(1,1,1)
+        u_add(0,2,1)
+        c_copy(1,0)
+        c_turn(1,3)
+        c_turn(1,2)
+        u_add(0,1,1)
+        sum_g(0,1,0,V)
+        prod_s(0,0,24,28)
+        sum_s(0,0,0,G)
+        c_quant(1,0)
+        u_add(0,1,0)
+        sum_s(0,0,1,G)
+        c_copy(1,3)
+        store(0,1,12,16)
+        c_quant(1,1)
+        c_copy(1,2)
+        r_mm(1,1,0)
+        store(0,1,4,8)
+        c_quant(1,3)
+        r_mm(1,0,0)
+        c_quant(1,2)
+        r_add(1,1,0)
+        r_add(1,0,0)
+        r_mm(1,0,1)
+        u_mm(0,2,0)
+        store(0,1,8,12)
+        u_add(0,3,0)
+        u_mm(0,0,0)
+        r_add(1,0,1)
+        prod_g(1,1,0,G)
+        u_add(0,2,0)
+        r_mm(1,1,1)
+        u_mm(0,0,1)
+        prod_s(1,0,12,16)
+        u_add(0,0,0)
+        prod_s(1,0,0,4)
+        store(0,0,4,8)
+        u_mm(1,0,1)
+        r_add(1,1,1)
+        prod_s(1,0,20,24)
+        store(0,0,12,16)
+        u_mm(1,1,1)
+        u_add(0,0,1)
+        sum_g(1,1,0,V)
+        u_add(1,0,1)
+        prod_s(1,0,8,12)
+        u_mm(1,3,1)
+        prod_s(1,0,16,20)
+        u_mm(1,0,0)
+        u_mm(1,2,1)
+        u_mm(1,1,0)
+        store(0,0,8,12)
+        u_mm(1,2,0)
+        store(0,0,0,4)
+        prod_s(1,0,24,28)
+        prod_s(1,0,4,8)
+        store(0,1,0,4)
+        prod_g(1,1,1,G)
+        u_add(1,1,1)
+        u_add(1,3,1)
+        u_mm(1,3,0)
+        sum_g(1,1,1,V)
+        prod_s(1,0,28,32)
+        u_add(1,2,1)
+        sum_s(1,0,1,G)
+        store(1,1,0,4)
+        store(1,1,4,8)
+        u_add(1,0,0)
+        sum_s(1,0,0,G)
+        u_add(1,1,0)
+        store(1,1,12,16)
+        u_add(1,2,0)
+        store(1,1,8,12)
+        store(1,0,0,4)
+        store(1,0,8,12)
+        u_add(1,3,0)
+        store(1,0,4,8)
+        store(1,0,12,16)

@@ -50,12 +50,12 @@ def tile_multiheadlatentattention_pb_w8_kernel(
         qd_planes = keep.tile([P, QC], U8, name="qd_planes", align_bytes=64)
         qu_planes = keep.tile([P, GC, NH * HD], U8, name="qu_planes", align_bytes=64)
         qr_planes = keep.tile([P, GC, NH * RD], U8, name="qr_planes", align_bytes=64)
-        bias_rows = keep.tile([P, 512], BF16, name="bias_rows")
+        bias_rows = keep.tile([P, 384], BF16, name="bias_rows")
         ident_b = keep.tile([P, P], BF16, name="ident_b")
         sc_rows = keep.tile([P, 512], F32, name="sc_rows")
         nc.vector.memset(sc_rows[:], 0.0)
-        nc.vector.memset(qd_planes[:].bitcast(I32), 0)
         nc.vector.memset(bias_rows[:], 0.0)
+        nc.vector.memset(qd_planes[:].bitcast(I32), 0)
         nc.vector.tensor_copy(out=ident_b[:], in_=ident[:])
         nc.vector.memset(qr_planes[:].rearrange("p g n -> p (g n)").bitcast(I32), 0)
         nc.vector.memset(qu_planes[:].rearrange("p g n -> p (g n)").bitcast(I32), 0)
@@ -92,20 +92,22 @@ def tile_multiheadlatentattention_pb_w8_kernel(
 
         load_x(0, 0)
         nc.sync.dma_start(out=sc_rows[0:GX, :], in_=x_scale.rearrange("a o (g k) -> (a o g) k", g=GX))
-        load_planes(qd_planes, W_qd_scales, GX)
-        w_qd = [load_words(W_qd_words, 0, QC, "w_qd0")]
-        load_x(0, 1)
         load_bias(b_qd, 0, 4)
+        load_planes(qd_planes, W_qd_scales, GX)
+        load_x(0, 1)
+        w_qd = [load_words(W_qd_words, 0, QC, "w_qd0")]
         w_qd.append(load_words(W_qd_words, 1, QC, "w_qd1"))
         load_x(1, 0)
         w_qd.append(load_words(W_qd_words, 2, QC, "w_qd2"))
         load_x(1, 1)
         w_qd.append(load_words(W_qd_words, 3, QC, "w_qd3"))
-        load_bias(b_qu, 4, 4)
-        load_bias(b_qr, 8, 2)
         load_block_planes(qr_planes, W_qr_scales)
+        br = keep.tile([P, NH * RD], BF16, name="br")
+        nc.sync.dma_start(out=br[:], in_=b_qr.partition_broadcast(P))
         w_qr = [load_words(W_qr_words, g, NH * RD, "w_qr%d" % g) for g in range(GC)]
         load_block_planes(qu_planes, W_qu_scales)
+        bu = keep.tile([P, NH * HD], BF16, name="bu")
+        nc.sync.dma_start(out=bu[:], in_=b_qu.partition_broadcast(P))
         w_qu = []
         for h in range(2):
             w = keep.tile([P, GC, 1024], U32, name="w_qu%d" % h, align_bytes=64)
@@ -113,8 +115,6 @@ def tile_multiheadlatentattention_pb_w8_kernel(
                               in_=W_qu_words[:, :, 1024 * h : 1024 * (h + 1), :].rearrange("g p n t -> p g (n t)").bitcast(I32))
             w_qu.append(w)
         bd = keep.tile([P, QC], BF16, name="bd")
-        bu = keep.tile([P, NH * HD], BF16, name="bu")
-        br = keep.tile([P, NH * RD], BF16, name="br")
 
         turns = keep.tile([P, NT, HALF], F32, name="turns")
         nc.gpsimd.tensor_scalar(turns[:, :, 0:1], pos[:].unsqueeze(2), 1.0 / (2.0 * math.pi), None, MULT)
@@ -156,13 +156,11 @@ def tile_multiheadlatentattention_pb_w8_kernel(
 
         def spread(row):
             turned["b", row] = new_turned()
-            cols = 384 if row < 4 else 512
-            nc.tensor.matmul(turned["b", row][:, 0:cols], lhsT=ident_b[:, row : row + 1].to_broadcast([P, P]),
-                             rhs=bias_rows[:, 0:cols], start=True, stop=True)
+            nc.tensor.matmul(turned["b", row][:, 0:384], lhsT=ident_b[:, row : row + 1].to_broadcast([P, P]),
+                             rhs=bias_rows[:], start=True, stop=True)
 
         def spread_copy(row):
-            tile, first, cols = (bd, 0, 384) if row < 4 else (bu, 4, 512) if row < 8 else (br, 8, 512)
-            nc.scalar.copy(out=tile[:, (row - first) * cols : (row - first + 1) * cols], in_=turned["b", row][:, 0:cols])
+            nc.scalar.copy(out=bd[:, 384 * row : 384 * row + 384], in_=turned["b", row][:, 0:384])
 
         def cast(b, g, engine):
             h, cols = g // 2, slice(512 * (g % 2), 512 * (g % 2) + 512)
@@ -181,12 +179,14 @@ def tile_multiheadlatentattention_pb_w8_kernel(
                 for u in range(2):
                     nc.tensor.transpose(turned[b, g][:, 256 * u + P * i : 256 * u + P * i + P], words[:, lo + u : lo + 256 : 2], ident[:])
 
-        def x_scale_v(b, g):
-            grouped[b, g] = stage.tile([P, NT * P, 4], BF16, name="xg", bufs=3, align_bytes=64)
+        def x_scale_v(b, g, i0=0, i1=NT):
+            if (b, g) not in grouped:
+                grouped[b, g] = stage.tile([P, NT * P, 4], BF16, name="xg", bufs=3, align_bytes=64)
+            rows, count = slice(P * i0, P * i1), P * (i1 - i0)
             nc.vector.tensor_tensor(
-                grouped[b, g][:].rearrange("p r (u e) -> p r u e", u=2),
-                turned[b, g][:].bitcast(BF16).rearrange("p (u r e) -> p r u e", u=2, e=2),
-                sc[:, g, :].rearrange("p (u e) -> p u e", u=2).unsqueeze(1).to_broadcast([P, NT * P, 2, 2]),
+                grouped[b, g][:, rows].rearrange("p r (u e) -> p r u e", u=2),
+                turned[b, g][:].bitcast(BF16).rearrange("p (u r e) -> p r u e", u=2, e=2)[:, rows],
+                sc[:, g, :].rearrange("p (u e) -> p u e", u=2).unsqueeze(1).to_broadcast([P, count, 2, 2]),
                 MULT,
             )
 
@@ -202,14 +202,15 @@ def tile_multiheadlatentattention_pb_w8_kernel(
             grouped[b, g] = stage.tile([P, NT * P, 4], BF16, name="xg", bufs=3, align_bytes=64)
             nc.gpsimd.tensor_tensor(grouped[b, g][:], lifted[b, g][:], sc[:, g, :].unsqueeze(1).to_broadcast([P, NT * P, 4]), MULT)
 
-        def quantize(tile, name):
-            codes = keep.tile([P, NT * P], U32, name="q" + name, align_bytes=64)
-            plane = keep.tile([P, NT * P], U8, name="s" + name, align_bytes=64)
-            nc.vector.quantize_mx(out=codes[:].bitcast(FP8X4), scales=plane[:], in_=tile[:].rearrange("p r k -> p (r k)"))
-            return codes, plane
-
-        def x_quant(b, g):
-            xq[b, g] = quantize(grouped[b, g], "x%d%d" % (b, g))
+        def x_quant(b, g, i0=0, i1=NT):
+            if (b, g) not in xq:
+                codes = keep.tile([P, NT * P], U32, name="qx%d%d" % (b, g), align_bytes=64)
+                plane = keep.tile([P, NT * P], U8, name="sx%d%d" % (b, g), align_bytes=64)
+                xq[b, g] = (codes, plane)
+            codes, plane = xq[b, g]
+            rows = slice(P * i0, P * i1)
+            nc.vector.quantize_mx(out=codes[:, rows].bitcast(FP8X4), scales=plane[:, rows],
+                                  in_=grouped[b, g][:, rows].rearrange("p r k -> p (r k)"))
 
         def mx(acc, operand, i, words, word_plane, start, stop):
             codes, plane = operand
@@ -336,208 +337,192 @@ def tile_multiheadlatentattention_pb_w8_kernel(
         GROUPS = [[[(0, 0), (1, 0)], [(0, 1), (1, 1)], [(0, 2), (1, 2)]],
                   [[(0, 0), (0, 1)], [(0, 2)], [(1, 0), (1, 1)], [(1, 2)]]]
 
-        cast(0,1,"s")
         scales_turn()
-        cast(0,0,"v")
-        cast(0,3,"s")
-        x_turn(0,0)
-        scales_copy()
-        x_scale_v(0,0)
-        x_turn(0,1)
-        angles(0)
-        x_quant(0,0)
-        cast(0,2,"v")
-        x_mm(0,0,0)
-        x_mm(0,0,1)
-        x_turn(0,3)
-        x_lift(0,3)
-        x_scale_v(0,1)
-        cast(1,1,"s")
-        x_quant(0,1)
-        x_turn(0,2)
-        cast(1,0,"s")
-        x_mm(0,1,0)
-        x_mm(0,1,1)
-        x_turn(1,1)
-        x_scale_v(0,2)
-        x_quant(0,2)
-        x_turn(1,0)
-        cast(1,3,"s")
-        x_mm(0,2,0)
-        x_mm(0,2,1)
-        x_scale_v(1,1)
-        cast(1,2,"s")
-        x_scale_g(0,3)
-        x_scale_v(1,0)
-        x_quant(0,3)
-        spread(1)
-        spread(0)
-        x_quant(1,1)
-        spread_copy(1)
-        x_mm(0,3,0)
         spread(2)
-        spread_copy(0)
-        c_add_v(0,0,0)
-        c_lift(0,0,1)
-        spread(3)
-        spread_copy(3)
+        cast(0,0,"v")
+        scales_copy()
+        x_turn(0,0)
+        cast(0,1,"s")
+        x_scale_v(0,0,0,1)
         spread_copy(2)
-        x_mm(0,3,1)
-        x_quant(1,0)
-        x_turn(1,3)
-        x_lift(1,3)
-        x_turn(1,2)
-        c_add_v(0,1,2)
-        c_add_v(0,0,2)
-        c_turn(0,2)
-        c_lift(0,1,0)
-        x_scale_v(1,2)
-        c_add_g(0,1,0)
-        x_mm(1,0,0)
-        spread(7)
-        c_add_g(0,0,1)
-        c_copy(0,2)
-        spread_copy(7)
+        spread(0)
+        x_scale_v(0,0,1,2)
+        spread_copy(0)
+        spread(3)
+        x_quant(0,0,1,2)
+        spread(1)
+        cast(0,2,"v")
+        spread_copy(3)
+        spread_copy(1)
+        x_turn(0,1)
+        x_quant(0,0,0,1)
+        x_turn(0,2)
+        x_scale_v(0,1)
+        cast(0,3,"s")
+        cast(1,0,"s")
+        angles(0)
+        x_mm(0,0,1)
+        x_quant(0,1)
+        x_turn(0,3)
+        x_mm(0,0,0)
+        x_scale_v(0,2)
+        x_mm(0,1,1)
         angles(1)
-        spread(5)
-        x_mm(1,1,0)
-        spread_copy(5)
-        spread(9)
-        x_scale_g(1,3)
-        spread(4)
-        c_add_v(0,1,1)
-        x_mm(1,0,1)
-        spread_copy(9)
-        spread_copy(4)
-        x_quant(1,2)
+        x_turn(1,0)
+        x_scale_v(0,3)
+        x_quant(0,2)
+        x_mm(0,1,0)
+        x_mm(0,2,1)
+        cast(1,1,"s")
+        x_quant(0,3)
+        cast(1,2,"s")
+        x_scale_v(1,0)
         angles(2)
+        x_mm(0,3,1)
+        x_mm(0,2,0)
+        x_quant(1,0)
+        x_mm(0,3,0)
+        x_turn(1,2)
+        c_add_v(0,1,0)
+        cast(1,3,"s")
+        c_add_v(0,1,1)
+        c_add_v(0,1,2)
+        c_add_v(0,0,1)
         c_turn(0,1)
+        x_mm(1,0,0)
         c_copy(0,1)
-        c_turn(0,0)
-        c_quant(0,2)
-        c_quant(0,1)
-        x_mm(1,2,0)
-        x_quant(1,3)
-        c_copy(0,0)
-        spread(6)
-        c_quant(0,0)
-        spread(8)
-        x_mm(1,3,0)
-        spread_copy(6)
-        r_mm(0,1,0)
         tables()
-        c_add_v(1,0,2)
-        spread_copy(8)
-        r_mm(0,0,0)
-        c_lift(1,0,1)
+        c_add_v(0,0,0)
+        x_scale_v(1,2)
+        c_add_v(0,0,2)
+        x_turn(1,1)
+        x_scale_v(1,1)
+        c_turn(0,0)
+        x_quant(1,1)
+        x_mm(1,0,1)
+        c_quant(0,1)
+        c_turn(0,2)
+        c_copy(0,0)
+        c_quant(0,0)
+        c_copy(0,2)
+        x_turn(1,3)
+        c_quant(0,2)
+        x_mm(1,1,0)
+        r_mm(0,1,0)
+        x_scale_v(1,3)
         r_add(0,1,0)
-        r_add(0,0,0)
-        prod_s(0,0,16,20)
-        c_add_v(1,0,0)
         r_mm(0,1,1)
-        prod_s(0,0,20,24)
-        r_mm(0,0,1)
-        x_mm(1,1,1)
-        x_mm(1,2,1)
+        x_quant(1,3)
         r_add(0,1,1)
-        x_mm(1,3,1)
-        prod_s(0,0,8,12)
-        r_add(0,0,1)
-        u_mm(0,3,1)
-        c_add_v(1,1,2)
-        prod_s(0,0,28,32)
-        u_mm(0,2,1)
-        prod_s(0,0,4,8)
-        c_add_g(1,0,1)
-        c_lift(1,1,1)
-        prod_s(0,0,12,16)
-        c_turn(1,1)
+        x_quant(1,2)
+        r_mm(0,0,0)
+        x_mm(1,1,1)
+        r_mm(0,0,1)
+        r_add(0,0,0)
         prod_g(0,1,1,G)
-        sum_g(0,1,1,V)
-        u_add(0,3,1)
-        c_turn(1,0)
-        u_mm(0,1,1)
-        prod_g(0,1,0,G)
+        x_mm(1,2,0)
+        x_mm(1,3,0)
+        r_add(0,0,1)
+        prod_s(0,0,20,24)
+        c_add_v(1,0,2)
+        c_add_v(1,0,0)
+        x_mm(1,2,1)
         prod_s(0,0,0,4)
-        c_add_v(1,1,0)
-        u_mm(0,1,0)
-        c_copy(1,1)
-        u_mm(0,3,0)
-        c_add_g(1,1,1)
-        u_add(0,2,1)
-        c_copy(1,0)
-        c_turn(1,3)
-        c_turn(1,2)
-        u_add(0,1,1)
-        sum_g(0,1,0,V)
+        x_mm(1,3,1)
+        prod_s(0,0,12,16)
+        prod_s(0,0,8,12)
         prod_s(0,0,24,28)
-        sum_s(0,0,0,G)
-        c_quant(1,0)
-        u_add(0,1,0)
-        sum_s(0,0,1,G)
+        prod_s(0,0,16,20)
+        c_add_v(1,0,1)
+        c_turn(1,1)
+        c_turn(1,0)
+        u_mm(0,2,1)
+        c_copy(1,1)
+        c_copy(1,0)
+        u_mm(0,0,1)
+        c_add_v(1,1,1)
+        prod_s(0,0,4,8)
+        c_add_v(1,1,2)
+        c_turn(1,3)
+        c_add_v(1,1,0)
         c_copy(1,3)
-        store(0,1,12,16)
         c_quant(1,1)
+        c_turn(1,2)
+        sum_g(0,1,1,G)
+        u_add(0,2,1)
+        u_add(0,0,1)
+        c_quant(1,0)
+        prod_g(0,1,0,G)
         c_copy(1,2)
-        r_mm(1,1,0)
-        store(0,1,4,8)
-        c_quant(1,3)
-        r_mm(1,0,0)
         c_quant(1,2)
+        c_quant(1,3)
+        u_mm(0,3,1)
+        prod_s(0,0,28,32)
+        sum_g(0,1,0,G)
+        u_add(0,3,1)
+        r_mm(1,1,0)
+        store(0,1,8,12)
+        r_mm(1,0,0)
+        store(0,1,0,4)
         r_add(1,1,0)
         r_add(1,0,0)
+        sum_s(0,0,1,G)
+        prod_s(1,0,4,8)
+        u_mm(0,1,0)
+        store(0,1,12,16)
         r_mm(1,0,1)
+        sum_s(0,0,0,G)
+        prod_s(1,0,28,32)
+        u_add(0,1,0)
+        u_mm(0,3,0)
+        store(0,0,4,8)
+        prod_s(1,0,24,28)
         u_mm(0,2,0)
-        store(0,1,8,12)
-        u_add(0,3,0)
-        u_mm(0,0,0)
+        u_mm(0,1,1)
+        prod_s(1,0,16,20)
         r_add(1,0,1)
+        u_add(0,3,0)
         prod_g(1,1,0,G)
         u_add(0,2,0)
-        r_mm(1,1,1)
-        u_mm(0,0,1)
-        prod_s(1,0,12,16)
-        u_add(0,0,0)
-        prod_s(1,0,0,4)
-        store(0,0,4,8)
-        u_mm(1,0,1)
-        r_add(1,1,1)
-        prod_s(1,0,20,24)
-        store(0,0,12,16)
-        u_mm(1,1,1)
-        u_add(0,0,1)
-        sum_g(1,1,0,V)
-        u_add(1,0,1)
         prod_s(1,0,8,12)
-        u_mm(1,3,1)
-        prod_s(1,0,16,20)
-        u_mm(1,0,0)
-        u_mm(1,2,1)
-        u_mm(1,1,0)
+        sum_g(1,1,0,G)
+        store(0,0,12,16)
         store(0,0,8,12)
-        u_mm(1,2,0)
-        store(0,0,0,4)
-        prod_s(1,0,24,28)
-        prod_s(1,0,4,8)
-        store(0,1,0,4)
-        prod_g(1,1,1,G)
+        u_mm(1,1,1)
+        u_add(0,1,1)
+        u_mm(0,0,0)
         u_add(1,1,1)
-        u_add(1,3,1)
-        u_mm(1,3,0)
-        sum_g(1,1,1,V)
-        prod_s(1,0,28,32)
-        u_add(1,2,1)
-        sum_s(1,0,1,G)
-        store(1,1,0,4)
+        u_mm(1,1,0)
+        u_mm(1,0,1)
+        store(0,1,4,8)
+        r_mm(1,1,1)
+        u_mm(1,2,0)
+        u_add(0,0,0)
         store(1,1,4,8)
-        u_add(1,0,0)
-        sum_s(1,0,0,G)
+        store(0,0,0,4)
+        u_add(1,0,1)
         u_add(1,1,0)
-        store(1,1,12,16)
+        u_mm(1,0,0)
+        prod_s(1,0,20,24)
+        u_mm(1,2,1)
+        store(1,1,0,4)
+        r_add(1,1,1)
+        u_mm(1,3,0)
+        prod_s(1,0,0,4)
         u_add(1,2,0)
-        store(1,1,8,12)
-        store(1,0,0,4)
-        store(1,0,8,12)
+        prod_s(1,0,12,16)
+        sum_s(1,0,0,G)
+        u_mm(1,3,1)
+        sum_s(1,0,1,G)
+        u_add(1,0,0)
         u_add(1,3,0)
         store(1,0,4,8)
+        store(1,0,8,12)
+        u_add(1,3,1)
+        store(1,0,0,4)
+        prod_g(1,1,1,G)
         store(1,0,12,16)
+        u_add(1,2,1)
+        sum_g(1,1,1,G)
+        store(1,1,12,16)
+        store(1,1,8,12)

@@ -80,7 +80,7 @@ def tile_multiheadlatentattention_pb_w8_kernel(
         def load_words(words, g, width, name):
             w = keep.tile([P, width], U32, name=name, align_bytes=64)
             nc.sync.dma_start(out=w[:].bitcast(I32), in_=words[g].rearrange("p n t -> p (n t)").bitcast(I32))
-            return w
+            return [w[:, 512 * n : 512 * n + 512] for n in range(width // 512)]
 
         def load_block_planes(planes, scales):
             for q in range(4):
@@ -94,26 +94,27 @@ def tile_multiheadlatentattention_pb_w8_kernel(
         nc.sync.dma_start(out=sc_rows[0:GX, :], in_=x_scale.rearrange("a o (g k) -> (a o g) k", g=GX))
         load_bias(b_qd, 0, 4)
         load_planes(qd_planes, W_qd_scales, GX)
-        load_x(0, 1)
         w_qd = [load_words(W_qd_words, 0, QC, "w_qd0")]
+        load_x(0, 1)
         w_qd.append(load_words(W_qd_words, 1, QC, "w_qd1"))
         load_x(1, 0)
         w_qd.append(load_words(W_qd_words, 2, QC, "w_qd2"))
         load_x(1, 1)
         w_qd.append(load_words(W_qd_words, 3, QC, "w_qd3"))
         load_block_planes(qr_planes, W_qr_scales)
-        br = keep.tile([P, NH * RD], BF16, name="br")
-        nc.sync.dma_start(out=br[:], in_=b_qr.partition_broadcast(P))
         w_qr = [load_words(W_qr_words, g, NH * RD, "w_qr%d" % g) for g in range(GC)]
+        br = keep.tile([P, NH * RD], BF16, name="br")
+        br_j = keep.tile([P, HALF, NH, 2], BF16, name="br_j")
+        nc.sync.dma_start(out=br[:], in_=b_qr.partition_broadcast(P))
         load_block_planes(qu_planes, W_qu_scales)
         bu = keep.tile([P, NH * HD], BF16, name="bu")
-        nc.sync.dma_start(out=bu[:], in_=b_qu.partition_broadcast(P))
         w_qu = []
         for h in range(2):
             w = keep.tile([P, GC, 1024], U32, name="w_qu%d" % h, align_bytes=64)
             nc.sync.dma_start(out=w[:].bitcast(I32),
                               in_=W_qu_words[:, :, 1024 * h : 1024 * (h + 1), :].rearrange("g p n t -> p g (n t)").bitcast(I32))
             w_qu.append(w)
+        nc.sync.dma_start(out=bu[:], in_=b_qu.partition_broadcast(P))
         bd = keep.tile([P, QC], BF16, name="bd")
 
         turns = keep.tile([P, NT, HALF], F32, name="turns")
@@ -171,13 +172,22 @@ def tile_multiheadlatentattention_pb_w8_kernel(
                 else:
                     nc.scalar.copy(out=dst, in_=src)
 
+        sorted_words = {}
+
+        def x_sort(b, g):
+            sorted_words[b, g] = stage.tile([P, NT, 2, P], F32, name="sorted_words")
+            lo = 256 * (g % 2)
+            nc.scalar.copy(out=sorted_words[b, g][:],
+                           in_=xb[b][g // 2][:].bitcast(F32)[:, :, lo : lo + 256].rearrange("p i (q u) -> p i u q", u=2))
+
         def x_turn(b, g):
             turned[b, g] = new_turned()
             lo = 256 * (g % 2)
             for i in range(NT):
                 words = xb[b][g // 2][:, i, :].bitcast(F32)
                 for u in range(2):
-                    nc.tensor.transpose(turned[b, g][:, 256 * u + P * i : 256 * u + P * i + P], words[:, lo + u : lo + 256 : 2], ident[:])
+                    nc.tensor.transpose(turned[b, g][:, 256 * u + P * i : 256 * u + P * i + P],
+                                        sorted_words[b, g][:, i, u] if (b, g) in sorted_words else words[:, lo + u : lo + 256 : 2], ident[:])
 
         def x_scale_v(b, g, i0=0, i1=NT):
             if (b, g) not in grouped:
@@ -223,7 +233,7 @@ def tile_multiheadlatentattention_pb_w8_kernel(
                 if (b, i, n) not in accs:
                     accs[b, i, n] = new_acc()
                 cols = slice(512 * n, 512 * n + 512)
-                mx(accs[b, i, n], xq[b, g], i, w_qd[g][:, cols], qd_planes[4 * g :, cols], g == 0, g == GX - 1)
+                mx(accs[b, i, n], xq[b, g], i, w_qd[g][n], qd_planes[4 * g :, cols], g == 0, g == GX - 1)
 
         def c_views(b, i, n):
             if (b, n) not in c_bf:
@@ -281,7 +291,17 @@ def tile_multiheadlatentattention_pb_w8_kernel(
             cols = slice(512 * n, 512 * n + 512)
             for g in range(GC):
                 operand, s = cq[b, i, g]
-                mx(accs["r", b, n, i], operand, s, w_qr[g][:, cols], qr_planes[:, g, cols], g == 0, g == GC - 1)
+                mx(accs["r", b, n, i], operand, s, w_qr[g][n], qr_planes[:, g, cols], g == 0, g == GC - 1)
+
+        def bias_sort():
+            S_.copy(out=br_j[:], in_=br[:].rearrange("p (h a j) -> p j h a", a=2, j=HALF))
+
+        def r_add_s(b, n, i):
+            if (b, i) not in q:
+                q[b, i] = stage.tile([P, HALF, NH, 2], F32, name="q_rot")
+            hs = slice(8 * n, 8 * n + 8)
+            nc.vector.tensor_tensor(q[b, i][:, :, hs, :], accs["r", b, n, i][:].rearrange("p (h a j) -> p j h a", a=2, j=HALF),
+                                    br_j[:, :, hs, :], ADD)
 
         def r_add(b, n, i):
             if (b, i) not in q:
@@ -295,7 +315,7 @@ def tile_multiheadlatentattention_pb_w8_kernel(
                 sa[b, i] = stage.tile([P, HALF, NH, 2], F32, name="sa")
             for j in range(lo, hi):
                 for dst, table in ((ca, cos_t), (sa, sin_t)):
-                    nc.scalar.activation(dst[b, i][:, j], q[b, i][:, :, :, j], COPY, scale=table[:, i, 1, j : j + 1])
+                    nc.scalar.activation(dst[b, i][:, j], q[b, i][:, j], COPY, scale=table[:, i, 1, j : j + 1])
 
         def sum_s(b, i, a, eng):
             eng.tensor_tensor(results[b][:, :, i, HD + HALF * a : HD + HALF * (a + 1)],
@@ -332,197 +352,206 @@ def tile_multiheadlatentattention_pb_w8_kernel(
             nc.scalar.activation(sin_t[:, :, 1], frac[:, 1], SIN, scale=2.0 * math.pi)
 
         def store(b, i, h0, h1):
-            nc.sync.dma_start(out=out[b, h0:h1].rearrange("h (p i) d -> p i h d", i=NT)[:, i], in_=results[b][:, h0:h1, i, :])
+            if i is None:
+                nc.sync.dma_start(out=out[b, h0:h1].rearrange("h (p i) d -> p h (i d)", i=NT),
+                                  in_=results[b][:, h0:h1].rearrange("p h i d -> p h (i d)"))
+            else:
+                nc.sync.dma_start(out=out[b, h0:h1].rearrange("h (p i) d -> p i h d", i=NT)[:, i], in_=results[b][:, h0:h1, i, :])
 
         GROUPS = [[[(0, 0), (1, 0)], [(0, 1), (1, 1)], [(0, 2), (1, 2)]],
                   [[(0, 0), (0, 1)], [(0, 2)], [(1, 0), (1, 1)], [(1, 2)]]]
 
         scales_turn()
-        spread(2)
         cast(0,0,"v")
-        scales_copy()
-        x_turn(0,0)
-        cast(0,1,"s")
-        x_scale_v(0,0,0,1)
-        spread_copy(2)
-        spread(0)
-        x_scale_v(0,0,1,2)
-        spread_copy(0)
-        spread(3)
-        x_quant(0,0,1,2)
         spread(1)
-        cast(0,2,"v")
-        spread_copy(3)
+        scales_copy()
+        cast(0,1,"s")
         spread_copy(1)
-        x_turn(0,1)
-        x_quant(0,0,0,1)
-        x_turn(0,2)
-        x_scale_v(0,1)
-        cast(0,3,"s")
-        cast(1,0,"s")
+        x_turn(0,0)
+        x_scale_v(0,0,0,1)
+        spread(2)
+        spread_copy(2)
+        x_scale_v(0,0,1,2)
+        spread(0)
         angles(0)
-        x_mm(0,0,1)
-        x_quant(0,1)
-        x_turn(0,3)
-        x_mm(0,0,0)
-        x_scale_v(0,2)
-        x_mm(0,1,1)
+        x_turn(0,1)
+        spread_copy(0)
         angles(1)
-        x_turn(1,0)
+        x_quant(0,0,1,2)
+        x_quant(0,0,0,1)
+        spread(3)
+        x_scale_v(0,1)
+        x_mm(0,0,1)
+        cast(0,2,"v")
+        cast(0,3,"s")
+        x_turn(0,3)
+        spread_copy(3)
+        x_turn(0,2)
+        x_quant(0,1)
+        x_mm(0,0,0)
+        cast(1,0,"s")
         x_scale_v(0,3)
+        x_mm(0,1,1)
+        x_scale_v(0,2)
+        x_sort(1,0)
+        x_turn(1,0)
+        x_quant(0,3)
         x_quant(0,2)
         x_mm(0,1,0)
-        x_mm(0,2,1)
-        cast(1,1,"s")
-        x_quant(0,3)
         cast(1,2,"s")
+        x_mm(0,2,1)
         x_scale_v(1,0)
         angles(2)
+        x_quant(1,0)
+        cast(1,1,"s")
         x_mm(0,3,1)
         x_mm(0,2,0)
-        x_quant(1,0)
-        x_mm(0,3,0)
-        x_turn(1,2)
         c_add_v(0,1,0)
-        cast(1,3,"s")
         c_add_v(0,1,1)
         c_add_v(0,1,2)
-        c_add_v(0,0,1)
-        c_turn(0,1)
+        x_mm(0,3,0)
         x_mm(1,0,0)
-        c_copy(0,1)
-        tables()
+        x_sort(1,1)
+        cast(1,3,"s")
         c_add_v(0,0,0)
-        x_scale_v(1,2)
-        c_add_v(0,0,2)
-        x_turn(1,1)
-        x_scale_v(1,1)
         c_turn(0,0)
-        x_quant(1,1)
+        c_copy(0,0)
+        x_sort(1,2)
+        c_add_v(0,0,1)
+        x_turn(1,1)
+        c_add_v(0,0,2)
+        tables()
         x_mm(1,0,1)
+        c_turn(0,1)
+        x_sort(1,3)
+        x_scale_v(1,1)
+        c_copy(0,1)
+        x_turn(1,2)
+        bias_sort()
+        x_quant(1,1)
+        x_mm(1,1,0)
+        x_scale_v(1,2)
+        x_quant(1,2)
         c_quant(0,1)
         c_turn(0,2)
-        c_copy(0,0)
+        x_turn(1,3)
         c_quant(0,0)
         c_copy(0,2)
-        x_turn(1,3)
         c_quant(0,2)
-        x_mm(1,1,0)
-        r_mm(0,1,0)
-        x_scale_v(1,3)
-        r_add(0,1,0)
-        r_mm(0,1,1)
-        x_quant(1,3)
-        r_add(0,1,1)
-        x_quant(1,2)
-        r_mm(0,0,0)
         x_mm(1,1,1)
+        x_scale_v(1,3)
         r_mm(0,0,1)
-        r_add(0,0,0)
-        prod_g(0,1,1,G)
+        r_add(0,0,1)
+        x_quant(1,3)
+        x_mm(1,2,1)
+        r_mm(0,0,0)
+        r_mm(0,1,0)
+        r_add_s(0,0,0)
+        r_add_s(0,1,0)
+        r_mm(0,1,1)
+        r_add(0,1,1)
         x_mm(1,2,0)
         x_mm(1,3,0)
-        r_add(0,0,1)
-        prod_s(0,0,20,24)
-        c_add_v(1,0,2)
-        c_add_v(1,0,0)
-        x_mm(1,2,1)
-        prod_s(0,0,0,4)
-        x_mm(1,3,1)
-        prod_s(0,0,12,16)
-        prod_s(0,0,8,12)
-        prod_s(0,0,24,28)
-        prod_s(0,0,16,20)
-        c_add_v(1,0,1)
-        c_turn(1,1)
-        c_turn(1,0)
-        u_mm(0,2,1)
-        c_copy(1,1)
-        c_copy(1,0)
-        u_mm(0,0,1)
-        c_add_v(1,1,1)
-        prod_s(0,0,4,8)
-        c_add_v(1,1,2)
-        c_turn(1,3)
-        c_add_v(1,1,0)
-        c_copy(1,3)
-        c_quant(1,1)
-        c_turn(1,2)
-        sum_g(0,1,1,G)
-        u_add(0,2,1)
-        u_add(0,0,1)
-        c_quant(1,0)
         prod_g(0,1,0,G)
-        c_copy(1,2)
-        c_quant(1,2)
-        c_quant(1,3)
+        x_mm(1,3,1)
+        prod_s(0,0,24,28)
+        c_add_v(1,0,0)
         u_mm(0,3,1)
-        prod_s(0,0,28,32)
-        sum_g(0,1,0,G)
-        u_add(0,3,1)
-        r_mm(1,1,0)
-        store(0,1,8,12)
-        r_mm(1,0,0)
-        store(0,1,0,4)
-        r_add(1,1,0)
-        r_add(1,0,0)
-        sum_s(0,0,1,G)
-        prod_s(1,0,4,8)
+        prod_s(0,0,0,4)
+        c_add_v(1,0,2)
+        prod_s(0,0,8,12)
+        c_turn(1,1)
+        c_add_v(1,0,1)
+        c_add_v(1,1,0)
+        c_turn(1,0)
         u_mm(0,1,0)
-        store(0,1,12,16)
-        r_mm(1,0,1)
-        sum_s(0,0,0,G)
-        prod_s(1,0,28,32)
-        u_add(0,1,0)
-        u_mm(0,3,0)
-        store(0,0,4,8)
-        prod_s(1,0,24,28)
-        u_mm(0,2,0)
+        prod_g(0,1,1,G)
+        prod_s(0,0,12,16)
+        prod_s(0,0,28,32)
+        sum_g(0,1,1,G)
+        sum_g(0,1,0,G)
+        c_add_v(1,1,2)
+        c_copy(1,1)
         u_mm(0,1,1)
-        prod_s(1,0,16,20)
-        r_add(1,0,1)
-        u_add(0,3,0)
-        prod_g(1,1,0,G)
-        u_add(0,2,0)
-        prod_s(1,0,8,12)
-        sum_g(1,1,0,G)
-        store(0,0,12,16)
-        store(0,0,8,12)
-        u_mm(1,1,1)
+        u_add(0,3,1)
+        prod_s(0,0,16,20)
+        c_add_v(1,1,1)
+        u_mm(0,2,1)
+        store(0,1,12,16)
+        u_add(0,1,0)
+        c_copy(1,0)
         u_add(0,1,1)
-        u_mm(0,0,0)
-        u_add(1,1,1)
-        u_mm(1,1,0)
-        u_mm(1,0,1)
+        c_turn(1,2)
+        c_quant(1,1)
         store(0,1,4,8)
+        prod_s(0,0,4,8)
+        c_turn(1,3)
+        u_mm(0,0,1)
+        c_copy(1,2)
+        c_quant(1,0)
+        u_add(0,2,1)
+        c_quant(1,2)
+        u_add(0,0,1)
+        r_mm(1,0,0)
+        prod_s(0,0,20,24)
+        sum_s(0,0,0,G)
+        c_copy(1,3)
+        r_add_s(1,0,0)
+        r_mm(1,1,0)
+        c_quant(1,3)
+        store(0,1,0,4)
         r_mm(1,1,1)
+        sum_s(0,0,1,G)
+        r_add_s(1,1,0)
+        u_mm(0,2,0)
+        r_add(1,1,1)
+        u_mm(0,3,0)
+        prod_s(1,0,20,24)
+        store(0,1,8,12)
+        store(0,0,4,8)
+        u_add(0,2,0)
+        r_mm(1,0,1)
+        u_mm(1,3,1)
+        prod_s(1,0,4,8)
+        u_mm(0,0,0)
+        prod_s(1,0,28,32)
+        prod_s(1,0,0,4)
+        u_mm(1,2,1)
+        prod_g(1,1,1,G)
+        prod_s(1,0,16,20)
+        u_add(0,3,0)
+        prod_s(1,0,8,12)
+        store(0,0,12,16)
+        prod_s(1,0,24,28)
+        prod_s(1,0,12,16)
+        u_mm(1,1,1)
+        r_add(1,0,1)
         u_mm(1,2,0)
+        u_mm(1,0,1)
+        u_add(1,3,1)
+        sum_g(1,1,1,V)
+        prod_g(1,1,0,G)
+        store(0,0,8,12)
         u_add(0,0,0)
-        store(1,1,4,8)
+        u_add(1,2,1)
+        u_add(1,1,1)
+        sum_g(1,1,0,V)
+        store(1,1,12,16)
+        sum_s(1,0,0,G)
+        u_mm(1,0,0)
+        sum_s(1,0,1,G)
+        u_add(1,2,0)
         store(0,0,0,4)
         u_add(1,0,1)
-        u_add(1,1,0)
-        u_mm(1,0,0)
-        prod_s(1,0,20,24)
-        u_mm(1,2,1)
-        store(1,1,0,4)
-        r_add(1,1,1)
-        u_mm(1,3,0)
-        prod_s(1,0,0,4)
-        u_add(1,2,0)
-        prod_s(1,0,12,16)
-        sum_s(1,0,0,G)
-        u_mm(1,3,1)
-        sum_s(1,0,1,G)
         u_add(1,0,0)
-        u_add(1,3,0)
-        store(1,0,4,8)
-        store(1,0,8,12)
-        u_add(1,3,1)
-        store(1,0,0,4)
-        prod_g(1,1,1,G)
-        store(1,0,12,16)
-        u_add(1,2,1)
-        sum_g(1,1,1,G)
-        store(1,1,12,16)
+        u_mm(1,3,0)
+        u_mm(1,1,0)
         store(1,1,8,12)
+        u_add(1,3,0)
+        store(1,1,4,8)
+        store(1,1,0,4)
+        store(1,0,8,12)
+        u_add(1,1,0)
+        store(1,0,4,8)
+        store(1,0,0,4)
+        store(1,0,12,16)

import math
from contextlib import ExitStack

import concourse.mybir as mybir
from concourse.masks import make_identity

F32 = mybir.dt.float32
BF16 = mybir.dt.bfloat16
I32 = mybir.dt.int32
U32 = mybir.dt.uint32
U8 = mybir.dt.uint8
FP8 = mybir.dt.float8_e4m3fn
FP8X4 = mybir.dt.float8_e4m3fn_x4
ADD = mybir.AluOpType.add
SUB = mybir.AluOpType.subtract
MULT = mybir.AluOpType.mult
SIN = mybir.ActivationFunctionType.Sin
COPY = mybir.ActivationFunctionType.Copy

P = 128
B, S, HID, NH, HD, RD, QC = 2, 256, 2048, 16, 128, 64, 1536
NT = S // P
GX = HID // 512
GC = QC // 512
HALF = RD // 2

FLOPS = 2 * B * S * (HID * QC + QC * NH * (HD + RD))


def tile_multiheadlatentattention_pb_w8_kernel(
    tc, x_bytes, x_scale, W_qd_words, W_qd_scales, b_qd, W_qu_words, W_qu_scales, b_qu,
    W_qr_words, W_qr_scales, b_qr, out,
):
    nc = tc.nc
    with ExitStack() as ctx:
        keep = ctx.enter_context(tc.tile_pool(name="keep", bufs=1))
        stage = ctx.enter_context(tc.tile_pool(name="stage", bufs=2))
        accp = ctx.enter_context(tc.psum_pool(name="accp", bufs=6))
        turnp = ctx.enter_context(tc.psum_pool(name="turnp", bufs=2))
        ctx.enter_context(tc.manual_schedule())

        pos = keep.tile([P, NT], F32, name="pos")
        nc.gpsimd.iota(pos[:], pattern=[[1, NT]], base=0, channel_multiplier=NT,
                       allow_small_or_imprecise_dtypes=True)
        warm = keep.tile([P, 1], F32, name="warm")
        nc.scalar.activation(warm[:], pos[:, 0:1], SIN, scale=0.0)
        ident = keep.tile([P, P], F32, name="ident")
        make_identity(nc, ident[:])

        qd_planes = keep.tile([P, QC], U8, name="qd_planes", align_bytes=64)
        qu_planes = keep.tile([P, GC, NH * HD], U8, name="qu_planes", align_bytes=64)
        qr_planes = keep.tile([P, GC, NH * RD], U8, name="qr_planes", align_bytes=64)
        bias_rows = keep.tile([P, 384], BF16, name="bias_rows")
        ident_b = keep.tile([P, P], BF16, name="ident_b")
        sc_rows = keep.tile([P, 512], F32, name="sc_rows")
        nc.vector.memset(sc_rows[:], 0.0)
        nc.vector.memset(bias_rows[:], 0.0)
        nc.vector.memset(qd_planes[:].bitcast(I32), 0)
        nc.vector.tensor_copy(out=ident_b[:], in_=ident[:])
        nc.vector.memset(qr_planes[:].rearrange("p g n -> p (g n)").bitcast(I32), 0)
        nc.vector.memset(qu_planes[:].rearrange("p g n -> p (g n)").bitcast(I32), 0)

        sc = keep.tile([P, GX, 4], F32, name="sc")

        x8 = [[keep.tile([P, NT, 1024], U8, name="x8_%d%d" % (b, h)) for h in range(2)] for b in range(B)]

        def load_x(b, h):
            nc.sync.dma_start(
                out=x8[b][h][:],
                in_=x_bytes[b].rearrange("(p i) k -> p i k", i=NT)[:, :, 1024 * h : 1024 * (h + 1)],
            )

        def load_planes(planes, scales, groups):
            for q in range(4):
                nc.sync.dma_start(
                    out=planes[32 * q : 32 * q + 4 * groups, :].bitcast(I32),
                    in_=scales[:, 4 * q : 4 * q + 4, :].bitcast(I32),
                )

        def load_words(words, g, width, name):
            w = keep.tile([P, width], U32, name=name, align_bytes=64)
            nc.sync.dma_start(out=w[:].bitcast(I32), in_=words[g].rearrange("p n t -> p (n t)").bitcast(I32))
            return [w[:, 512 * n : 512 * n + 512] for n in range(width // 512)]

        def load_block_planes(planes, scales):
            for q in range(4):
                nc.sync.dma_start(out=planes[32 * q : 32 * q + 4].bitcast(I32),
                                  in_=scales[:, 4 * q : 4 * q + 4, :].rearrange("g q n -> q g n").bitcast(I32))

        def load_bias(bias, row, rows):
            nc.sync.dma_start(out=bias_rows[row : row + rows, 0 : bias.shape[0] // rows], in_=bias.rearrange("(r c) -> r c", r=rows))

        load_x(0, 0)
        nc.sync.dma_start(out=sc_rows[0:GX, :], in_=x_scale.rearrange("a o (g k) -> (a o g) k", g=GX))
        load_bias(b_qd, 0, 4)
        load_planes(qd_planes, W_qd_scales, GX)
        w_qd = [load_words(W_qd_words, 0, QC, "w_qd0")]
        load_x(0, 1)
        w_qd.append(load_words(W_qd_words, 1, QC, "w_qd1"))
        load_x(1, 0)
        w_qd.append(load_words(W_qd_words, 2, QC, "w_qd2"))
        load_x(1, 1)
        w_qd.append(load_words(W_qd_words, 3, QC, "w_qd3"))
        load_block_planes(qr_planes, W_qr_scales)
        w_qr = [load_words(W_qr_words, g, NH * RD, "w_qr%d" % g) for g in range(GC)]
        br = keep.tile([P, NH * RD], BF16, name="br")
        br_j = keep.tile([P, HALF, NH, 2], BF16, name="br_j")
        nc.sync.dma_start(out=br[:], in_=b_qr.partition_broadcast(P))
        load_block_planes(qu_planes, W_qu_scales)
        bu = keep.tile([P, NH * HD], BF16, name="bu")
        w_qu = []
        for h in range(2):
            w = keep.tile([P, GC, 1024], U32, name="w_qu%d" % h, align_bytes=64)
            nc.sync.dma_start(out=w[:].bitcast(I32),
                              in_=W_qu_words[:, :, 1024 * h : 1024 * (h + 1), :].rearrange("g p n t -> p g (n t)").bitcast(I32))
            w_qu.append(w)
        nc.sync.dma_start(out=bu[:], in_=b_qu.partition_broadcast(P))
        bd = keep.tile([P, QC], BF16, name="bd")

        turns = keep.tile([P, NT, HALF], F32, name="turns")
        nc.gpsimd.tensor_scalar(turns[:, :, 0:1], pos[:].unsqueeze(2), 1.0 / (2.0 * math.pi), None, MULT)
        width = 1
        while width < HALF:
            nc.gpsimd.tensor_scalar(turns[:, :, width : 2 * width], turns[:, :, 0:width],
                                    10000.0 ** (-width / HALF), None, MULT)
            width *= 2
        phase = keep.tile([P, 2, NT, HALF], F32, name="phase")
        nc.gpsimd.tensor_scalar(phase[:, 0], turns[:], 0.25, None, ADD)
        nc.gpsimd.tensor_scalar(phase[:, 1], turns[:], 0.0, None, ADD)
        whole_i = keep.tile([P, 2, NT, HALF], I32, name="whole_i")
        whole = keep.tile([P, 2, NT, HALF], F32, name="whole")
        frac = keep.tile([P, 2, NT, HALF], F32, name="frac")
        cos_t = keep.tile([P, NT, 2, HALF], F32, name="cos_t")
        sin_t = keep.tile([P, NT, 2, HALF], F32, name="sin_t")

        xb = [[keep.tile([P, NT, 1024], BF16, name="xb_%d%d" % (b, h), align_bytes=64) for h in range(2)] for b in range(B)]
        turned, lifted, grouped, xq, cq, accs, c_raw, c_bf = {}, {}, {}, {}, {}, {}, {}, {}
        q, ca, sa = {}, {}, {}
        results = [keep.tile([P, NH, NT, HD + RD], F32, name="res%d" % b) for b in range(B)]
        V, G, S_ = nc.vector, nc.gpsimd, nc.scalar

        def new_turned():
            bank = turnp.tile([P, 512], F32, name="bank")
            return bank

        def new_acc():
            acc = accp.tile([P, 512], F32, name="acc")
            return acc

        def scales_turn():
            turned["s"] = new_turned()
            for t in range(4):
                nc.tensor.transpose(turned["s"][:, P * t : P * t + P], sc_rows[:, t::4], ident[:])

        def scales_copy():
            nc.vector.tensor_copy(out=sc[:], in_=turned["s"][:].rearrange("p (t g) -> p g t", t=4)[:, 0:GX, :])

        def spread(row):
            turned["b", row] = new_turned()
            nc.tensor.matmul(turned["b", row][:, 0:384], lhsT=ident_b[:, row : row + 1].to_broadcast([P, P]),
                             rhs=bias_rows[:], start=True, stop=True)

        def spread_copy(row):
            nc.scalar.copy(out=bd[:, 384 * row : 384 * row + 384], in_=turned["b", row][:, 0:384])

        def cast(b, g, engine):
            h, cols = g // 2, slice(512 * (g % 2), 512 * (g % 2) + 512)
            for i in range(NT):
                src, dst = x8[b][h][:, i, cols].bitcast(FP8), xb[b][h][:, i, cols]
                if engine == "v":
                    nc.vector.tensor_copy(out=dst, in_=src)
                else:
                    nc.scalar.copy(out=dst, in_=src)

        sorted_words = {}

        def x_sort(b, g):
            sorted_words[b, g] = stage.tile([P, NT, 2, P], F32, name="sorted_words")
            lo = 256 * (g % 2)
            nc.scalar.copy(out=sorted_words[b, g][:],
                           in_=xb[b][g // 2][:].bitcast(F32)[:, :, lo : lo + 256].rearrange("p i (q u) -> p i u q", u=2))

        def x_turn(b, g):
            turned[b, g] = new_turned()
            lo = 256 * (g % 2)
            for i in range(NT):
                words = xb[b][g // 2][:, i, :].bitcast(F32)
                for u in range(2):
                    nc.tensor.transpose(turned[b, g][:, 256 * u + P * i : 256 * u + P * i + P],
                                        sorted_words[b, g][:, i, u] if (b, g) in sorted_words else words[:, lo + u : lo + 256 : 2], ident[:])

        def x_scale_v(b, g, i0=0, i1=NT):
            if (b, g) not in grouped:
                grouped[b, g] = stage.tile([P, NT * P, 4], BF16, name="xg", bufs=3, align_bytes=64)
            rows, count = slice(P * i0, P * i1), P * (i1 - i0)
            nc.vector.tensor_tensor(
                grouped[b, g][:, rows].rearrange("p r (u e) -> p r u e", u=2),
                turned[b, g][:].bitcast(BF16).rearrange("p (u r e) -> p r u e", u=2, e=2)[:, rows],
                sc[:, g, :].rearrange("p (u e) -> p u e", u=2).unsqueeze(1).to_broadcast([P, count, 2, 2]),
                MULT,
            )

        def words_out(dst, bank):
            nc.scalar.copy(out=dst[:].rearrange("p r k -> p (r k)").bitcast(F32).rearrange("p (r u) -> p r u", u=2),
                           in_=bank[:].rearrange("p (u r) -> p r u", u=2))

        def x_lift(b, g):
            lifted[b, g] = stage.tile([P, NT * P, 4], BF16, name="xw", align_bytes=64)
            words_out(lifted[b, g], turned[b, g])

        def x_scale_g(b, g):
            grouped[b, g] = stage.tile([P, NT * P, 4], BF16, name="xg", bufs=3, align_bytes=64)
            nc.gpsimd.tensor_tensor(grouped[b, g][:], lifted[b, g][:], sc[:, g, :].unsqueeze(1).to_broadcast([P, NT * P, 4]), MULT)

        def x_quant(b, g, i0=0, i1=NT):
            if (b, g) not in xq:
                codes = keep.tile([P, NT * P], U32, name="qx%d%d" % (b, g), align_bytes=64)
                plane = keep.tile([P, NT * P], U8, name="sx%d%d" % (b, g), align_bytes=64)
                xq[b, g] = (codes, plane)
            codes, plane = xq[b, g]
            rows = slice(P * i0, P * i1)
            nc.vector.quantize_mx(out=codes[:, rows].bitcast(FP8X4), scales=plane[:, rows],
                                  in_=grouped[b, g][:, rows].rearrange("p r k -> p (r k)"))

        def mx(acc, operand, i, words, word_plane, start, stop):
            codes, plane = operand
            rows = slice(i * P, (i + 1) * P)
            nc.tensor.matmul_mx(out=acc[:], lhsT=codes[:, rows].bitcast(FP8X4), lhsT_scale=plane[:, rows],
                                rhs=words.bitcast(FP8X4), rhs_scale=word_plane, start=start, stop=stop)

        def x_mm(b, g, i):
            for n in range(GC):
                if (b, i, n) not in accs:
                    accs[b, i, n] = new_acc()
                cols = slice(512 * n, 512 * n + 512)
                mx(accs[b, i, n], xq[b, g], i, w_qd[g][n], qd_planes[4 * g :, cols], g == 0, g == GX - 1)

        def c_views(b, i, n):
            if (b, n) not in c_bf:
                c_bf[b, n] = keep.tile([P, NT, 512], BF16, name="c%d%d" % (b, n), align_bytes=64)
            return (c_bf[b, n][:, i, :].rearrange("p (u k e) -> p u k e", u=2, e=2),
                    bd[:, 512 * n : 512 * n + 512].rearrange("p (k u e) -> p u k e", u=2, e=2))

        def c_add_v(b, i, n):
            dst, bias = c_views(b, i, n)
            nc.vector.tensor_tensor(dst, accs[b, i, n][:].rearrange("p (k u e) -> p u k e", u=2, e=2), bias, ADD)

        def c_lift(b, i, n):
            c_raw[b, i, n] = stage.tile([P, 512], F32, name="c_raw", bufs=3)
            nc.scalar.copy(out=c_raw[b, i, n][:], in_=accs[b, i, n][:])

        def c_add_g(b, i, n):
            dst, bias = c_views(b, i, n)
            nc.gpsimd.tensor_tensor(dst, c_raw[b, i, n][:].rearrange("p (k u e) -> p u k e", u=2, e=2), bias, ADD)

        def c_turn(b, k):
            turned["c", b, k] = new_turned()
            for s, (i, n) in enumerate(GROUPS[b][k]):
                for u in range(2):
                    nc.tensor.transpose(turned["c", b, k][:, 256 * s + P * u : 256 * s + P * u + P],
                                        c_bf[b, n][:, i, 256 * u : 256 * u + 256].bitcast(F32), ident[:])

        def c_copy(b, k):
            count = len(GROUPS[b][k])
            grouped["c", b, k] = stage.tile([P, count * P, 4], BF16, name="cg%d" % count, bufs=3, align_bytes=64)
            nc.scalar.copy(
                out=grouped["c", b, k][:].rearrange("p r k -> p (r k)").bitcast(F32).rearrange("p (c r u) -> p c r u", c=count, u=2),
                in_=turned["c", b, k][:, 0 : 256 * count].rearrange("p (c u r) -> p c r u", c=count, u=2))

        def c_quant(b, k):
            count = len(GROUPS[b][k])
            codes = keep.tile([P, count * P], U32, name="qc%d%d" % (b, k), align_bytes=64)
            plane = keep.tile([P, count * P], U8, name="sc%d%d" % (b, k), align_bytes=64)
            nc.vector.quantize_mx(out=codes[:].bitcast(FP8X4), scales=plane[:], in_=grouped["c", b, k][:].rearrange("p r k -> p (r k)"))
            for s, (i, n) in enumerate(GROUPS[b][k]):
                cq[b, i, n] = (codes, plane), s

        def u_mm(b, n, i):
            accs["u", b, n, i] = new_acc()
            cols, half = slice(512 * n, 512 * n + 512), slice(512 * (n % 2), 512 * (n % 2) + 512)
            for g in range(GC):
                operand, s = cq[b, i, g]
                mx(accs["u", b, n, i], operand, s, w_qu[n // 2][:, g, half], qu_planes[:, g, cols], g == 0, g == GC - 1)

        def u_add(b, n, i):
            nc.vector.tensor_tensor(results[b][:, 4 * n : 4 * n + 4, i, 0:HD], accs["u", b, n, i][:].rearrange("p (h d) -> p h d", d=HD),
                                    bu[:, 512 * n : 512 * n + 512].rearrange("p (h d) -> p h d", d=HD), ADD)

        def r_mm(b, n, i):
            accs["r", b, n, i] = new_turned()
            cols = slice(512 * n, 512 * n + 512)
            for g in range(GC):
                operand, s = cq[b, i, g]
                mx(accs["r", b, n, i], operand, s, w_qr[g][n], qr_planes[:, g, cols], g == 0, g == GC - 1)

        def bias_sort():
            S_.copy(out=br_j[:], in_=br[:].rearrange("p (h a j) -> p j h a", a=2, j=HALF))

        def r_add_s(b, n, i):
            if (b, i) not in q:
                q[b, i] = stage.tile([P, HALF, NH, 2], F32, name="q_rot")
            hs = slice(8 * n, 8 * n + 8)
            nc.vector.tensor_tensor(q[b, i][:, :, hs, :], accs["r", b, n, i][:].rearrange("p (h a j) -> p j h a", a=2, j=HALF),
                                    br_j[:, :, hs, :], ADD)

        def r_add(b, n, i):
            if (b, i) not in q:
                q[b, i] = stage.tile([P, NH, 2, HALF], F32, name="q_rot")
            nc.vector.tensor_tensor(q[b, i][:, 8 * n : 8 * n + 8].rearrange("p h a j -> p (h a j)"), accs["r", b, n, i][:],
                                    br[:, 512 * n : 512 * n + 512], ADD)

        def prod_s(b, i, lo, hi):
            if (b, i) not in ca:
                ca[b, i] = stage.tile([P, HALF, NH, 2], F32, name="ca")
                sa[b, i] = stage.tile([P, HALF, NH, 2], F32, name="sa")
            for j in range(lo, hi):
                for dst, table in ((ca, cos_t), (sa, sin_t)):
                    nc.scalar.activation(dst[b, i][:, j], q[b, i][:, j], COPY, scale=table[:, i, 1, j : j + 1])

        def sum_s(b, i, a, eng):
            eng.tensor_tensor(results[b][:, :, i, HD + HALF * a : HD + HALF * (a + 1)],
                              ca[b, i][:, :, :, a].rearrange("p j h -> p h j"),
                              sa[b, i][:, :, :, 1 - a].rearrange("p j h -> p h j"), ADD if a else SUB)

        def prod_g(b, i, n, eng):
            if (b, i) not in ca:
                ca[b, i] = stage.tile([P, NH, 2, HALF], F32, name="ca")
                sa[b, i] = stage.tile([P, NH, 2, HALF], F32, name="sa")
            hs = slice(8 * n, 8 * n + 8)
            eng.tensor_tensor(ca[b, i][:, hs].rearrange("p h a j -> p h (a j)"), q[b, i][:, hs].rearrange("p h a j -> p h (a j)"),
                              cos_t[:, i].rearrange("p a j -> p (a j)").unsqueeze(1).to_broadcast([P, 8, RD]), MULT)
            for a in range(2):
                eng.tensor_tensor(sa[b, i][:, hs, a, :], q[b, i][:, hs, 1 - a, :],
                                  sin_t[:, i, a, :].unsqueeze(1).to_broadcast([P, 8, HALF]), MULT)

        def sum_g(b, i, n, eng):
            hs = slice(8 * n, 8 * n + 8)
            eng.tensor_tensor(results[b][:, hs, i, HD:], ca[b, i][:, hs].rearrange("p h a j -> p h (a j)"),
                              sa[b, i][:, hs].rearrange("p h a j -> p h (a j)"), ADD)

        def angles(k):
            if k == 0:
                nc.vector.tensor_copy(out=whole_i[:], in_=phase[:])
            elif k == 1:
                nc.vector.tensor_copy(out=whole[:], in_=whole_i[:])
            else:
                nc.vector.tensor_tensor(frac[:], phase[:], whole[:], SUB)

        def tables():
            nc.scalar.activation(cos_t[:], frac[:, 0].unsqueeze(2).to_broadcast([P, NT, 2, HALF]), SIN, scale=2.0 * math.pi)
            nc.scalar.activation(sin_t[:, :, 0], frac[:, 1], SIN, scale=-2.0 * math.pi)
            nc.scalar.activation(sin_t[:, :, 1], frac[:, 1], SIN, scale=2.0 * math.pi)

        def store(b, i, h0, h1):
            if i is None:
                nc.sync.dma_start(out=out[b, h0:h1].rearrange("h (p i) d -> p h (i d)", i=NT),
                                  in_=results[b][:, h0:h1].rearrange("p h i d -> p h (i d)"))
            else:
                nc.sync.dma_start(out=out[b, h0:h1].rearrange("h (p i) d -> p i h d", i=NT)[:, i], in_=results[b][:, h0:h1, i, :])

        GROUPS = [[[(0, 0), (1, 0)], [(0, 1), (1, 1)], [(0, 2), (1, 2)]],
                  [[(0, 0), (0, 1)], [(0, 2)], [(1, 0), (1, 1)], [(1, 2)]]]

        scales_turn()
        cast(0,0,"v")
        spread(1)
        scales_copy()
        cast(0,1,"s")
        spread_copy(1)
        x_turn(0,0)
        x_scale_v(0,0,0,1)
        spread(2)
        spread_copy(2)
        x_scale_v(0,0,1,2)
        spread(0)
        angles(0)
        x_turn(0,1)
        spread_copy(0)
        angles(1)
        x_quant(0,0,1,2)
        x_quant(0,0,0,1)
        spread(3)
        x_scale_v(0,1)
        x_mm(0,0,1)
        cast(0,2,"v")
        cast(0,3,"s")
        x_turn(0,3)
        spread_copy(3)
        x_turn(0,2)
        x_quant(0,1)
        x_mm(0,0,0)
        cast(1,0,"s")
        x_scale_v(0,3)
        x_mm(0,1,1)
        x_scale_v(0,2)
        x_sort(1,0)
        x_turn(1,0)
        x_quant(0,3)
        x_quant(0,2)
        x_mm(0,1,0)
        cast(1,2,"s")
        x_mm(0,2,1)
        x_scale_v(1,0)
        angles(2)
        x_quant(1,0)
        cast(1,1,"s")
        x_mm(0,3,1)
        x_mm(0,2,0)
        c_add_v(0,1,0)
        c_add_v(0,1,1)
        c_add_v(0,1,2)
        x_mm(0,3,0)
        x_mm(1,0,0)
        x_sort(1,1)
        cast(1,3,"s")
        c_add_v(0,0,0)
        c_turn(0,0)
        c_copy(0,0)
        x_sort(1,2)
        c_add_v(0,0,1)
        x_turn(1,1)
        c_add_v(0,0,2)
        tables()
        x_mm(1,0,1)
        c_turn(0,1)
        x_sort(1,3)
        x_scale_v(1,1)
        c_copy(0,1)
        x_turn(1,2)
        bias_sort()
        x_quant(1,1)
        x_mm(1,1,0)
        x_scale_v(1,2)
        x_quant(1,2)
        c_quant(0,1)
        c_turn(0,2)
        x_turn(1,3)
        c_quant(0,0)
        c_copy(0,2)
        c_quant(0,2)
        x_mm(1,1,1)
        x_scale_v(1,3)
        r_mm(0,0,1)
        r_add(0,0,1)
        x_quant(1,3)
        x_mm(1,2,1)
        r_mm(0,0,0)
        r_mm(0,1,0)
        r_add_s(0,0,0)
        r_add_s(0,1,0)
        r_mm(0,1,1)
        r_add(0,1,1)
        x_mm(1,2,0)
        x_mm(1,3,0)
        prod_g(0,1,0,G)
        x_mm(1,3,1)
        prod_s(0,0,24,28)
        c_add_v(1,0,0)
        u_mm(0,3,1)
        prod_s(0,0,0,4)
        c_add_v(1,0,2)
        prod_s(0,0,8,12)
        c_turn(1,1)
        c_add_v(1,0,1)
        c_add_v(1,1,0)
        c_turn(1,0)
        u_mm(0,1,0)
        prod_g(0,1,1,G)
        prod_s(0,0,12,16)
        prod_s(0,0,28,32)
        sum_g(0,1,1,G)
        sum_g(0,1,0,G)
        c_add_v(1,1,2)
        c_copy(1,1)
        u_mm(0,1,1)
        u_add(0,3,1)
        prod_s(0,0,16,20)
        c_add_v(1,1,1)
        u_mm(0,2,1)
        store(0,1,12,16)
        u_add(0,1,0)
        c_copy(1,0)
        u_add(0,1,1)
        c_turn(1,2)
        c_quant(1,1)
        store(0,1,4,8)
        prod_s(0,0,4,8)
        c_turn(1,3)
        u_mm(0,0,1)
        c_copy(1,2)
        c_quant(1,0)
        u_add(0,2,1)
        c_quant(1,2)
        u_add(0,0,1)
        r_mm(1,0,0)
        prod_s(0,0,20,24)
        sum_s(0,0,0,G)
        c_copy(1,3)
        r_add_s(1,0,0)
        r_mm(1,1,0)
        c_quant(1,3)
        store(0,1,0,4)
        r_mm(1,1,1)
        sum_s(0,0,1,G)
        r_add_s(1,1,0)
        u_mm(0,2,0)
        r_add(1,1,1)
        u_mm(0,3,0)
        prod_s(1,0,20,24)
        store(0,1,8,12)
        store(0,0,4,8)
        u_add(0,2,0)
        r_mm(1,0,1)
        u_mm(1,3,1)
        prod_s(1,0,4,8)
        u_mm(0,0,0)
        prod_s(1,0,28,32)
        prod_s(1,0,0,4)
        u_mm(1,2,1)
        prod_g(1,1,1,G)
        prod_s(1,0,16,20)
        u_add(0,3,0)
        prod_s(1,0,8,12)
        store(0,0,12,16)
        prod_s(1,0,24,28)
        prod_s(1,0,12,16)
        u_mm(1,1,1)
        r_add(1,0,1)
        u_mm(1,2,0)
        u_mm(1,0,1)
        u_add(1,3,1)
        sum_g(1,1,1,V)
        prod_g(1,1,0,G)
        store(0,0,8,12)
        u_add(0,0,0)
        u_add(1,2,1)
        u_add(1,1,1)
        sum_g(1,1,0,V)
        store(1,1,12,16)
        sum_s(1,0,0,G)
        u_mm(1,0,0)
        sum_s(1,0,1,G)
        u_add(1,2,0)
        store(0,0,0,4)
        u_add(1,0,1)
        u_add(1,0,0)
        u_mm(1,3,0)
        u_mm(1,1,0)
        store(1,1,8,12)
        u_add(1,3,0)
        store(1,1,4,8)
        store(1,1,0,4)
        store(1,0,8,12)
        u_add(1,1,0)
        store(1,0,4,8)
        store(1,0,0,4)
        store(1,0,12,16)
